import numpy as np
import ml_dtypes


def mxq(x, axis, fmt="e4m3"):
    dtype, down = {"e4m3": (ml_dtypes.float8_e4m3fn, 7), "e5m2": (ml_dtypes.float8_e5m2, 14)}[fmt]
    v = np.moveaxis(np.asarray(x, np.float32).astype(ml_dtypes.bfloat16).astype(np.float64), axis, -1)
    blocks = v.reshape(v.shape[:-1] + (-1, 32))
    amax = np.abs(blocks).max(-1, keepdims=True)
    byte = np.maximum(np.where(amax > 0, np.frexp(amax)[1] - 1 + 127, 0) - down, 1)
    scale = np.exp2(byte - 127.0)
    codes = (blocks / scale).astype(np.float32).astype(dtype).astype(np.float64)
    return np.moveaxis((codes * scale).reshape(v.shape), -1, axis)


WIDE = False


def mx_kscale(k):
    if not WIDE:
        return np.ones(k)
    levels = np.array([10, -10, 5, -5, 0])
    a = np.random.permutation(np.resize(levels, k // 512 * 4)).reshape(k // 512, 4)
    idx = np.arange(k)
    return np.exp2(a[idx // 512, idx % 128 // 32])


BF16 = ml_dtypes.bfloat16


def bf(x):
    return np.asarray(x, np.float32).astype(BF16)


def f64(x):
    return np.asarray(x).astype(np.float64)


B, N, W, D = 2, 8192, 512, 128
NW = N // W
NEG = -1.0e30


def setup_inputs():
    s = np.array(mx_kscale(N), dtype=np.float64)
    s[np.arange(N) % W < D] = s.max()
    a = np.log2(s)
    q = np.random.standard_normal((B, N, D)) / np.sqrt(D)
    ko = np.random.standard_normal((B, N, D))
    kp = np.random.standard_normal((B, N - W, D))
    q[:, :, 0] = np.log(2.0)
    ko[:, :, 0] += a
    kp[:, :, 0] += a[:N - W]
    v = np.random.standard_normal((B, N, D)) * 3.0 * (s.max() / s)[:, None]
    return {"q_rot": bf(q), "k_own": bf(ko), "k_prev": bf(kp), "v": bf(v)}


def reference(q_rot, k_own, k_prev, v):
    q = f64(q_rot).reshape(B, NW, W, D)
    ko = f64(k_own).reshape(B, NW, W, D)
    kp = f64(k_prev).reshape(B, NW - 1, W, D)
    vq = mxq(f64(v), 1, "e4m3")
    pos = np.arange(W)
    later = pos[:, None] < pos[None, :]
    s_own = np.where(later, NEG, q @ ko.transpose(0, 1, 3, 2))
    s_prev = q[:, 1:] @ kp.transpose(0, 1, 3, 2)
    s0 = s_own[:, 0]
    e0 = np.exp(s0 - s0.max(-1, keepdims=True))
    outs = [(mxq(e0, 2, "e4m3") @ vq[:, :W]) / e0.sum(-1, keepdims=True)]
    s = np.concatenate([s_prev, s_own[:, 1:]], axis=-1)
    e = np.exp(s - s.max(-1, keepdims=True))
    eq = mxq(e, 3, "e4m3")
    for t in range(1, NW):
        outs.append((eq[:, t - 1] @ vq[:, (t - 1) * W:(t + 1) * W]) / e[:, t - 1].sum(-1, keepdims=True))
    return np.concatenate(outs, axis=1)

@@ -1,0 +1,354 @@
+from contextlib import ExitStack
+
+import concourse.mybir as mybir
+from concourse.masks import make_identity
+
+BF16 = mybir.dt.bfloat16
+F32 = mybir.dt.float32
+U32 = mybir.dt.uint32
+U8 = mybir.dt.uint8
+FP8X4 = mybir.dt.float8_e4m3fn_x4
+ALU = mybir.AluOpType
+ACT = mybir.ActivationFunctionType
+AXIS = mybir.AxisListType
+
+B, N, W, D = 2, 8192, 512, 128
+P = 128
+NW = N // W
+QT = W // P
+TILES = B * NW * QT
+HALF = W // 2
+PREV, OWN, QUERY = 0, 1, 2
+NEG = -1.0e30
+CHUNK = 4
+CHUNKS = NW // CHUNK
+LOAD_AHEAD = 2
+E_SLOTS = 2
+S_BANKS = 5
+
+FLOPS = 2 * 2 * B * (W * W + (NW - 1) * W * 2 * W) * D
+
+
+def tile_localattention_pa_t_kernel(tc, q_rot, k_own, k_prev, v, out):
+    nc = tc.nc
+    q_rows = q_rot.flatten_outer_dims()
+    k_rows = {OWN: k_own.flatten_outer_dims(), PREV: k_prev.flatten_outer_dims()}
+    k_seq_rows = {OWN: N, PREV: N - W}
+    v_rows = v.flatten_outer_dims()
+    out_rows = out.flatten_outer_dims()
+
+    with ExitStack() as ctx:
+        const = ctx.enter_context(tc.tile_pool(name="const", bufs=1))
+        turned_pool = ctx.enter_context(tc.tile_pool(name="turned_pool", bufs=3))
+        work = ctx.enter_context(tc.tile_pool(name="work", bufs=3))
+        small = ctx.enter_context(tc.tile_pool(name="small", bufs=6))
+        psum_s = ctx.enter_context(tc.psum_pool(name="psum_s", bufs=S_BANKS))
+        psum_e = ctx.enter_context(tc.psum_pool(name="psum_e", bufs=1))
+        psum_t = ctx.enter_context(tc.psum_pool(name="psum_t", bufs=1))
+        psum_o = ctx.enter_context(tc.psum_pool(name="psum_o", bufs=1))
+
+        ident_bf = const.tile([P, P], BF16)
+        make_identity(nc, ident_bf[:])
+        ident_f32 = const.tile([P, P], F32)
+        make_identity(nc, ident_f32[:])
+
+        mask_f32 = const.tile([P, P], F32)
+        nc.gpsimd.memset(mask_f32[:], 0.0)
+        nc.gpsimd.affine_select(
+            out=mask_f32[:],
+            in_=mask_f32[:],
+            compare_op=ALU.is_ge,
+            fill=NEG,
+            base=0,
+            pattern=[[-1, P]],
+            channel_multiplier=1,
+        )
+        mask_bf = const.tile([P, 2, P // 2], BF16)
+        nc.vector.tensor_copy(
+            out=mask_bf[:].rearrange("r u (p c) -> r u p c", c=2),
+            in_=mask_f32[:].rearrange("r (p u c) -> r u p c", u=2, c=2),
+        )
+
+        e_tiles = [
+            [const.tile([P, 2 * W], BF16, name="e_%d_%d" % (slot, i)) for i in range(QT)]
+            for slot in range(E_SLOTS)
+        ]
+        for slot in range(E_SLOTS):
+            for i in range(QT - 1):
+                e_view = e_tiles[slot][i][:].rearrange("q (s u c) -> q s u c", s=2, u=2)
+                nc.gpsimd.memset(e_view[:, OWN, :, (P // 2) * (i + 1) :], 0.0)
+
+        v_codes = const.tile([P, B * NW, D], U32, align_bytes=64)
+        v_scales = const.tile([P, B * NW, D], U8, align_bytes=64)
+
+        loaded = {}
+
+        def load_chunk(chunk):
+            if chunk >= B * CHUNKS:
+                return
+            b, c = divmod(chunk, CHUNKS)
+            for s in (OWN, PREV):
+                windows = min(CHUNK, k_seq_rows[s] // W - c * CHUNK)
+                row0 = b * k_seq_rows[s] + c * CHUNK * W
+                k_view = k_rows[s][row0 : row0 + windows * W, :].rearrange(
+                    "(wh a u c) d -> u c a wh d", a=P // 2, u=2, c=2
+                )
+                k_raw = const.tile([P, 2, 2 * CHUNK, D], BF16, name="k_raw_%d_%d" % (s, chunk))
+                for u in range(2):
+                    for c2 in range(2):
+                        nc.sync.dma_start(out=k_raw[c2:P:2, u, 0 : 2 * windows, :], in_=k_view[u, c2])
+                loaded[(s, chunk)] = k_raw
+                if s == OWN:
+                    row0 = b * N + c * CHUNK * W
+                    q_raw = const.tile([P, CHUNK * QT, D], BF16, name="q_raw_%d" % chunk)
+                    nc.sync.dma_start(
+                        out=q_raw[:],
+                        in_=q_rows[row0 : row0 + CHUNK * W, :].rearrange("(a r) d -> r a d", r=P),
+                    )
+                    loaded[(QUERY, chunk)] = q_raw
+            row0 = b * N + c * CHUNK * W
+            v_raw = const.tile([P, CHUNK, 4, D], BF16, name="v_raw_%d" % chunk)
+            nc.sync.dma_start(
+                out=v_raw[:],
+                in_=v_rows[row0 : row0 + CHUNK * W, :].rearrange("(w p j) d -> p w j d", p=P, j=4),
+            )
+            loaded[("v", chunk)] = v_raw
+
+        def parts_of(g):
+            return [OWN] if g % NW == 0 else [PREV, OWN]
+
+        def columns(s, i):
+            return HALF if s == PREV else (P // 2) * (i + 1)
+
+        turned = {}
+        rowsums = {}
+        recips = {}
+        outputs = {}
+        live = {}
+
+        def prepare_transposes(n):
+            gn, j = n // QT + 1, n % QT
+            if not 0 <= gn < B * NW:
+                return
+            if j == 0 and gn % CHUNK == 0:
+                load_chunk(gn // CHUNK + LOAD_AHEAD)
+            b, t = divmod(gn, NW)
+            u, h = divmod(j, 2)
+            t_ps = psum_t.tile([P, 3, P], BF16)
+            for s in parts_of(gn):
+                w = t - 1 + s
+                k_raw = loaded[(s, b * CHUNKS + w // CHUNK)]
+                nc.tensor.transpose(t_ps[:, s, :], k_raw[:, u, 2 * (w % CHUNK) + h, :], ident_bf[:])
+            q_raw = loaded[(QUERY, gn // CHUNK)]
+            nc.tensor.transpose(t_ps[:, QUERY, :], q_raw[:, (gn % CHUNK) * QT + j, :], ident_bf[:])
+            live[("t_ps", n)] = t_ps
+
+        def prepare_copy(n):
+            gn, j = n // QT + 1, n % QT
+            if not 0 <= gn < B * NW:
+                return
+            if j == 0:
+                turned[gn] = turned_pool.tile([P, 3, W], BF16, name="turned")
+            first = parts_of(gn)[0]
+            nc.vector.tensor_copy(
+                out=turned[gn][:, first:, j * P : (j + 1) * P], in_=live[("t_ps", n)][:, first:, :]
+            )
+
+        def prepare_v(n):
+            gn, j = n // QT + 1, n % QT
+            if not 0 <= gn < B * NW:
+                return
+            if j == 0:
+                v_grouped = work.tile([P, D, 4], BF16, align_bytes=64)
+                v_raw = loaded[("v", gn // CHUNK)]
+                nc.vector.tensor_copy(
+                    out=v_grouped[:], in_=v_raw[:, gn % CHUNK, :, :].rearrange("p j d -> p d j")
+                )
+                live[("v_grouped", gn)] = v_grouped
+            if j == 1:
+                nc.vector.quantize_mx(
+                    out=v_codes[:, gn, :].bitcast(FP8X4),
+                    scales=v_scales[:, gn, :],
+                    in_=live[("v_grouped", gn)][:].rearrange("p d j -> p (d j)"),
+                )
+
+        def scores(n, s):
+            g, i = divmod(n, QT)
+            if not 0 <= n < TILES or s not in parts_of(g):
+                return
+            cols = columns(s, i)
+            s_ps = psum_s.tile([P, 2, HALF], F32)
+            nc.tensor.matmul(
+                s_ps[:, :, 0:cols],
+                lhsT=turned[g][:, QUERY, i * P : (i + 1) * P],
+                rhs=turned[g][:, s, :].rearrange("d (u c) -> d u c", u=2)[:, :, 0:cols],
+                start=True,
+                stop=(s == PREV),
+            )
+            if s == OWN:
+                nc.tensor.matmul(
+                    s_ps[:, :, cols - P // 2 : cols],
+                    lhsT=ident_bf[:],
+                    rhs=mask_bf[:],
+                    start=False,
+                    stop=True,
+                )
+            live[("s_ps", s, n)] = s_ps
+
+        def row_max(n, s):
+            g, i = divmod(n, QT)
+            if not 0 <= n < TILES or s not in parts_of(g):
+                return
+            if s == parts_of(g)[0]:
+                live[("rowmax", n)] = small.tile([P, 2], F32, name="rowmax")
+            nc.vector.tensor_reduce(
+                out=live[("rowmax", n)][:, s : s + 1],
+                in_=live[("s_ps", s, n)][:, :, 0 : columns(s, i)],
+                axis=AXIS.XY,
+                op=ALU.max,
+            )
+
+        def negate_max(n):
+            if not 0 <= n < TILES:
+                return
+            rowmax = live[("rowmax", n)]
+            negmax = small.tile([P, 1], F32)
+            if len(parts_of(n // QT)) == 2:
+                nc.vector.tensor_scalar(
+                    out=negmax[:],
+                    in0=rowmax[:, PREV : PREV + 1],
+                    scalar1=rowmax[:, OWN : OWN + 1],
+                    scalar2=-1.0,
+                    op0=ALU.max,
+                    op1=ALU.mult,
+                )
+            else:
+                nc.vector.tensor_scalar(
+                    out=negmax[:], in0=rowmax[:, OWN : OWN + 1], scalar1=-1.0, scalar2=None, op0=ALU.mult
+                )
+            live[("negmax", n)] = negmax
+
+        def exponentials(n):
+            if not 0 <= n < TILES:
+                return
+            g, i = divmod(n, QT)
+            if i == 0:
+                rowsums[g] = small.tile([P, QT, 2], F32, name="rowsum")
+            e_view = e_tiles[g % E_SLOTS][i][:].rearrange("q (s u c) -> q s u c", s=2, u=2)
+            for s in parts_of(g):
+                cols = columns(s, i)
+                nc.scalar.activation(
+                    out=e_view[:, s, :, 0:cols],
+                    in_=live[("s_ps", s, n)][:, :, 0:cols],
+                    func=ACT.Exp,
+                    bias=live[("negmax", n)][:],
+                    scale=1.0,
+                    accum_out=rowsums[g][:, i, s : s + 1],
+                )
+
+        def transpose_e(n):
+            if not 0 <= n < TILES:
+                return
+            g, i = divmod(n, QT)
+            e_words = e_tiles[g % E_SLOTS][i][:].bitcast(F32)
+            eT_ps = psum_e.tile([P, 2, 2, P], F32)
+            for s in parts_of(g):
+                for u in range(2):
+                    word0 = (2 * s + u) * P
+                    nc.tensor.transpose(eT_ps[:, s, u, :], e_words[:, word0 : word0 + P], ident_f32[:])
+            live[("eT_ps", n)] = eT_ps
+
+        def regroup_e(n):
+            if not 0 <= n < TILES:
+                return
+            first = parts_of(n // QT)[0]
+            grouped = work.tile([P, 2 * P * 4], BF16, align_bytes=64)
+            grouped_words = grouped[:].bitcast(F32).rearrange("p (s q u) -> p s q u", s=2, u=2)
+            nc.scalar.copy(
+                out=grouped_words[:, first:, :, :],
+                in_=live[("eT_ps", n)][:, first:, :, :].rearrange("p s u q -> p s q u"),
+            )
+            live[("grouped", n)] = grouped
+
+        def quantise_e(n):
+            if not 0 <= n < TILES:
+                return
+            first = parts_of(n // QT)[0]
+            e_codes = work.tile([P, 2 * P], U32, align_bytes=64)
+            e_scales = work.tile([P, 2 * P], U8, align_bytes=64)
+            nc.vector.quantize_mx(
+                out=e_codes[:, first * P :].bitcast(FP8X4),
+                scales=e_scales[:, first * P :],
+                in_=live[("grouped", n)][:, first * P * 4 :],
+            )
+            live[("e_codes", n)] = e_codes
+            live[("e_scales", n)] = e_scales
+
+        def multiply_v(n):
+            if not 0 <= n < TILES:
+                return
+            g, i = divmod(n, QT)
+            if i == 0:
+                outputs[g] = psum_o.tile([P, QT, D], F32, name="o_ps")
+            for s in parts_of(g):
+                nc.tensor.matmul_mx(
+                    out=outputs[g][:, i, :],
+                    lhsT=live[("e_codes", n)][:, s * P : (s + 1) * P].bitcast(FP8X4),
+                    lhsT_scale=live[("e_scales", n)][:, s * P : (s + 1) * P],
+                    rhs=v_codes[:, g - 1 + s, :].bitcast(FP8X4),
+                    rhs_scale=v_scales[:, g - 1 + s, :],
+                    start=(s == parts_of(g)[0]),
+                    stop=(s == OWN),
+                )
+
+        def sum_rows(n):
+            g, i = divmod(n, QT)
+            if not 0 <= n < TILES or i != QT - 1:
+                return
+            total = small.tile([P, QT], F32)
+            nc.vector.tensor_reduce(
+                out=total[:], in_=rowsums[g][:, :, parts_of(g)[0] :], axis=AXIS.X, op=ALU.add
+            )
+            live[("total", g)] = total
+
+        def invert_sums(n):
+            g, i = divmod(n, QT)
+            if not 0 <= n < TILES or i != QT - 1:
+                return
+            recips[g] = small.tile([P, QT], F32, name="recip")
+            nc.vector.reciprocal(out=recips[g][:], in_=live[("total", g)][:])
+
+        def divide_and_store(n):
+            g, i = divmod(n, QT)
+            if not 0 <= n < TILES or i != QT - 1:
+                return
+            o_sb = work.tile([P, QT, D], F32)
+            for a in range(QT):
+                nc.scalar.activation(
+                    out=o_sb[:, a, :], in_=outputs[g][:, a, :], func=ACT.Copy, scale=recips[g][:, a : a + 1]
+                )
+            nc.sync.dma_start(
+                out=out_rows[g * W : (g + 1) * W, :].rearrange("(a r) d -> r a d", r=P), in_=o_sb[:]
+            )
+
+        for chunk in range(LOAD_AHEAD):
+            load_chunk(chunk)
+
+        with tc.manual_schedule():
+            for k in range(-QT - 2, TILES + 4):
+                prepare_transposes(k + 2)
+                transpose_e(k - 1)
+                scores(k + 2, PREV)
+                multiply_v(k - 3)
+                scores(k + 2, OWN)
+                row_max(k + 1, PREV)
+                prepare_copy(k + 2)
+                sum_rows(k - 1)
+                row_max(k + 1, OWN)
+                quantise_e(k - 2)
+                negate_max(k + 1)
+                prepare_v(k + 2)
+                invert_sums(k - 1)
+                exponentials(k)
+                regroup_e(k - 1)
+                divide_and_store(k - 3)

@@ -214,7 +214,7 @@ def tile_localattention_pa_t_kernel(tc, q_rot, k_own, k_prev, v, out):
             rowmax = live[("rowmax", n)]
             negmax = small.tile([P, 1], F32)
             if len(parts_of(n // QT)) == 2:
-                nc.vector.tensor_scalar(
+                nc.gpsimd.tensor_scalar(
                     out=negmax[:],
                     in0=rowmax[:, PREV : PREV + 1],
                     scalar1=rowmax[:, OWN : OWN + 1],
@@ -223,8 +223,13 @@ def tile_localattention_pa_t_kernel(tc, q_rot, k_own, k_prev, v, out):
                     op1=ALU.mult,
                 )
             else:
-                nc.vector.tensor_scalar(
-                    out=negmax[:], in0=rowmax[:, OWN : OWN + 1], scalar1=-1.0, scalar2=None, op0=ALU.mult
+                nc.gpsimd.tensor_scalar(
+                    out=negmax[:],
+                    in0=rowmax[:, OWN : OWN + 1],
+                    scalar1=-1.0,
+                    scalar2=0.0,
+                    op0=ALU.mult,
+                    op1=ALU.add,
                 )
             live[("negmax", n)] = negmax
 
@@ -323,10 +328,12 @@ def tile_localattention_pa_t_kernel(tc, q_rot, k_own, k_prev, v, out):
             if not 0 <= n < TILES or i != QT - 1:
                 return
             o_sb = work.tile([P, QT, D], F32)
-            for a in range(QT):
-                nc.scalar.activation(
-                    out=o_sb[:, a, :], in_=outputs[g][:, a, :], func=ACT.Copy, scale=recips[g][:, a : a + 1]
-                )
+            nc.vector.tensor_tensor(
+                out=o_sb[:],
+                in0=outputs[g][:],
+                in1=recips[g][:].unsqueeze(2).to_broadcast([P, QT, D]),
+                op=ALU.mult,
+            )
             nc.sync.dma_start(
                 out=out_rows[g * W : (g + 1) * W, :].rearrange("(a r) d -> r a d", r=P), in_=o_sb[:]
             )
@@ -346,9 +353,9 @@ def tile_localattention_pa_t_kernel(tc, q_rot, k_own, k_prev, v, out):
                 sum_rows(k - 1)
                 row_max(k + 1, OWN)
                 quantise_e(k - 2)
-                negate_max(k + 1)
                 prepare_v(k + 2)
                 invert_sums(k - 1)
+                divide_and_store(k - 3)
+                negate_max(k + 1)
                 exponentials(k)
                 regroup_e(k - 1)
-                divide_and_store(k - 3)

@@ -20,7 +20,7 @@ TILES = B * NW * QT
 HALF = W // 2
 PREV, OWN, QUERY = 0, 1, 2
 NEG = -1.0e30
-CHUNK = 4
+CHUNK = 2
 CHUNKS = NW // CHUNK
 LOAD_AHEAD = 2
 E_SLOTS = 2
@@ -162,7 +162,8 @@ def tile_localattention_pa_t_kernel(tc, q_rot, k_own, k_prev, v, out):
                 v_grouped = work.tile([P, D, 4], BF16, align_bytes=64)
                 v_raw = loaded[("v", gn // CHUNK)]
                 nc.vector.tensor_copy(
-                    out=v_grouped[:], in_=v_raw[:, gn % CHUNK, :, :].rearrange("p j d -> p d j")
+                    out=v_grouped[:].rearrange("p (m i) j -> p m j i", i=4),
+                    in_=v_raw[:, gn % CHUNK, :, :].rearrange("p j (m i) -> p m j i", i=4),
                 )
                 live[("v_grouped", gn)] = v_grouped
             if j == 1:
@@ -310,18 +311,21 @@ def tile_localattention_pa_t_kernel(tc, q_rot, k_own, k_prev, v, out):
             g, i = divmod(n, QT)
             if not 0 <= n < TILES or i != QT - 1:
                 return
-            total = small.tile([P, QT], F32)
-            nc.vector.tensor_reduce(
-                out=total[:], in_=rowsums[g][:, :, parts_of(g)[0] :], axis=AXIS.X, op=ALU.add
-            )
-            live[("total", g)] = total
+            if len(parts_of(g)) == 2:
+                total = small.tile([P, QT], F32)
+                nc.gpsimd.tensor_tensor(
+                    out=total[:], in0=rowsums[g][:, :, PREV], in1=rowsums[g][:, :, OWN], op=ALU.add
+                )
+                live[("total", g)] = total[:]
+            else:
+                live[("total", g)] = rowsums[g][:, :, OWN]
 
         def invert_sums(n):
             g, i = divmod(n, QT)
             if not 0 <= n < TILES or i != QT - 1:
                 return
             recips[g] = small.tile([P, QT], F32, name="recip")
-            nc.vector.reciprocal(out=recips[g][:], in_=live[("total", g)][:])
+            nc.vector.reciprocal(out=recips[g][:], in_=live[("total", g)])
 
         def divide_and_store(n):
             g, i = divmod(n, QT)
@@ -349,13 +353,13 @@ def tile_localattention_pa_t_kernel(tc, q_rot, k_own, k_prev, v, out):
                 multiply_v(k - 3)
                 scores(k + 2, OWN)
                 row_max(k + 1, PREV)
-                prepare_copy(k + 2)
-                sum_rows(k - 1)
                 row_max(k + 1, OWN)
                 quantise_e(k - 2)
+                prepare_copy(k + 2)
                 prepare_v(k + 2)
-                invert_sums(k - 1)
+                invert_sums(k - 2)
                 divide_and_store(k - 3)
                 negate_max(k + 1)
+                sum_rows(k - 1)
                 exponentials(k)
                 regroup_e(k - 1)

@@ -154,24 +154,32 @@ def tile_localattention_pa_t_kernel(tc, q_rot, k_own, k_prev, v, out):
                 out=turned[gn][:, first:, j * P : (j + 1) * P], in_=live[("t_ps", n)][:, first:, :]
             )
 
-        def prepare_v(n):
+        def interleave_v(n):
             gn, j = n // QT + 1, n % QT
             if not 0 <= gn < B * NW:
                 return
             if j == 0:
-                v_grouped = work.tile([P, D, 4], BF16, align_bytes=64)
-                v_raw = loaded[("v", gn // CHUNK)]
-                nc.vector.tensor_copy(
-                    out=v_grouped[:].rearrange("p (m i) j -> p m j i", i=4),
-                    in_=v_raw[:, gn % CHUNK, :, :].rearrange("p j (m i) -> p m j i", i=4),
-                )
-                live[("v_grouped", gn)] = v_grouped
-            if j == 1:
-                nc.vector.quantize_mx(
-                    out=v_codes[:, gn, :].bitcast(FP8X4),
-                    scales=v_scales[:, gn, :],
-                    in_=live[("v_grouped", gn)][:].rearrange("p d j -> p (d j)"),
-                )
+                live[("v_grouped", gn)] = work.tile([P, D, 4], BF16, align_bytes=64, name="v_grouped")
+            v_raw = loaded[("v", gn // CHUNK)]
+            features = slice(j * (D // QT), (j + 1) * (D // QT))
+            nc.gpsimd.tensor_scalar(
+                out=live[("v_grouped", gn)][:, features, :],
+                in0=v_raw[:, gn % CHUNK, :, features].rearrange("p j d -> p d j"),
+                scalar1=1.0,
+                scalar2=0.0,
+                op0=ALU.mult,
+                op1=ALU.add,
+            )
+
+        def quantise_v(n):
+            gn, j = n // QT, n % QT
+            if not 0 <= gn < B * NW or j != 0:
+                return
+            nc.vector.quantize_mx(
+                out=v_codes[:, gn, :].bitcast(FP8X4),
+                scales=v_scales[:, gn, :],
+                in_=live[("v_grouped", gn)][:].rearrange("p d j -> p (d j)"),
+            )
 
         def scores(n, s):
             g, i = divmod(n, QT)
@@ -356,10 +364,11 @@ def tile_localattention_pa_t_kernel(tc, q_rot, k_own, k_prev, v, out):
                 row_max(k + 1, OWN)
                 quantise_e(k - 2)
                 prepare_copy(k + 2)
-                prepare_v(k + 2)
+                quantise_v(k + 2)
                 invert_sums(k - 2)
                 divide_and_store(k - 3)
                 negate_max(k + 1)
                 sum_rows(k - 1)
+                interleave_v(k + 2)
                 exponentials(k)
                 regroup_e(k - 1)

@@ -143,16 +143,18 @@ def tile_localattention_pa_t_kernel(tc, q_rot, k_own, k_prev, v, out):
             nc.tensor.transpose(t_ps[:, QUERY, :], q_raw[:, (gn % CHUNK) * QT + j, :], ident_bf[:])
             live[("t_ps", n)] = t_ps
 
-        def prepare_copy(n):
+        def prepare_copy(n, engine):
             gn, j = n // QT + 1, n % QT
-            if not 0 <= gn < B * NW:
+            if not 0 <= gn < B * NW or (j % 2 == 1) != (engine == "scalar"):
                 return
             if j == 0:
                 turned[gn] = turned_pool.tile([P, 3, W], BF16, name="turned")
             first = parts_of(gn)[0]
-            nc.vector.tensor_copy(
-                out=turned[gn][:, first:, j * P : (j + 1) * P], in_=live[("t_ps", n)][:, first:, :]
-            )
+            quarter = turned[gn][:, first:, j * P : (j + 1) * P]
+            if engine == "scalar":
+                nc.scalar.copy(out=quarter, in_=live[("t_ps", n)][:, first:, :])
+            else:
+                nc.vector.tensor_copy(out=quarter, in_=live[("t_ps", n)][:, first:, :])
 
         def interleave_v(n):
             gn, j = n // QT + 1, n % QT
@@ -363,7 +365,7 @@ def tile_localattention_pa_t_kernel(tc, q_rot, k_own, k_prev, v, out):
                 row_max(k + 1, PREV)
                 row_max(k + 1, OWN)
                 quantise_e(k - 2)
-                prepare_copy(k + 2)
+                prepare_copy(k + 2, "vector")
                 quantise_v(k + 2)
                 invert_sums(k - 2)
                 divide_and_store(k - 3)
@@ -371,4 +373,5 @@ def tile_localattention_pa_t_kernel(tc, q_rot, k_own, k_prev, v, out):
                 sum_rows(k - 1)
                 interleave_v(k + 2)
                 exponentials(k)
+                prepare_copy(k + 2, "scalar")
                 regroup_e(k - 1)

@@ -134,6 +134,8 @@ def tile_localattention_pa_t_kernel(tc, q_rot, k_own, k_prev, v, out):
                 load_chunk(gn // CHUNK + LOAD_AHEAD)
             b, t = divmod(gn, NW)
             u, h = divmod(j, 2)
+            if j == 0:
+                turned[gn] = turned_pool.tile([P, 3, W], BF16, name="turned")
             t_ps = psum_t.tile([P, 3, P], BF16)
             for s in parts_of(gn):
                 w = t - 1 + s
@@ -145,10 +147,8 @@ def tile_localattention_pa_t_kernel(tc, q_rot, k_own, k_prev, v, out):
 
         def prepare_copy(n, engine):
             gn, j = n // QT + 1, n % QT
-            if not 0 <= gn < B * NW or (j % 2 == 1) != (engine == "scalar"):
+            if not 0 <= gn < B * NW or (j == 0) != (engine == "scalar"):
                 return
-            if j == 0:
-                turned[gn] = turned_pool.tile([P, 3, W], BF16, name="turned")
             first = parts_of(gn)[0]
             quarter = turned[gn][:, first:, j * P : (j + 1) * P]
             if engine == "scalar":

@@ -20,6 +20,7 @@ TILES = B * NW * QT
 HALF = W // 2
 PREV, OWN, QUERY = 0, 1, 2
 NEG = -1.0e30
+LOWEST = -3.0e38
 CHUNK = 2
 CHUNKS = NW // CHUNK
 LOAD_AHEAD = 2
@@ -49,11 +50,9 @@ def tile_localattention_pa_t_kernel(tc, q_rot, k_own, k_prev, v, out):
 
         ident_bf = const.tile([P, P], BF16)
         make_identity(nc, ident_bf[:])
-        ident_f32 = const.tile([P, P], F32)
-        make_identity(nc, ident_f32[:])
 
         mask_f32 = const.tile([P, P], F32)
-        nc.gpsimd.memset(mask_f32[:], 0.0)
+        nc.vector.memset(mask_f32[:], 0.0)
         nc.gpsimd.affine_select(
             out=mask_f32[:],
             in_=mask_f32[:],
@@ -68,6 +67,8 @@ def tile_localattention_pa_t_kernel(tc, q_rot, k_own, k_prev, v, out):
             out=mask_bf[:].rearrange("r u (p c) -> r u p c", c=2),
             in_=mask_f32[:].rearrange("r (p u c) -> r u p c", u=2, c=2),
         )
+        ident_f32 = const.tile([P, P], F32)
+        make_identity(nc, ident_f32[:])
 
         e_tiles = [
             [const.tile([P, 2 * W], BF16, name="e_%d_%d" % (slot, i)) for i in range(QT)]
@@ -76,7 +77,7 @@ def tile_localattention_pa_t_kernel(tc, q_rot, k_own, k_prev, v, out):
         for slot in range(E_SLOTS):
             for i in range(QT - 1):
                 e_view = e_tiles[slot][i][:].rearrange("q (s u c) -> q s u c", s=2, u=2)
-                nc.gpsimd.memset(e_view[:, OWN, :, (P // 2) * (i + 1) :], 0.0)
+                nc.vector.memset(e_view[:, OWN, :, (P // 2) * (i + 1) :], 0.0)
 
         v_codes = const.tile([P, B * NW, D], U32, align_bytes=64)
         v_scales = const.tile([P, B * NW, D], U8, align_bytes=64)
@@ -88,31 +89,38 @@ def tile_localattention_pa_t_kernel(tc, q_rot, k_own, k_prev, v, out):
                 return
             b, c = divmod(chunk, CHUNKS)
             for s in (OWN, PREV):
-                windows = min(CHUNK, k_seq_rows[s] // W - c * CHUNK)
-                row0 = b * k_seq_rows[s] + c * CHUNK * W
-                k_view = k_rows[s][row0 : row0 + windows * W, :].rearrange(
-                    "(wh a u c) d -> u c a wh d", a=P // 2, u=2, c=2
+                loaded[(s, chunk)] = const.tile([P, 2, 2 * CHUNK, D], BF16, name="k_raw_%d_%d" % (s, chunk))
+            loaded[(QUERY, chunk)] = const.tile([P, CHUNK * QT, D], BF16, name="q_raw_%d" % chunk)
+            loaded[("v", chunk)] = const.tile([P, CHUNK, 4, D], BF16, name="v_raw_%d" % chunk)
+            step = 1 if chunk == 0 else CHUNK
+            for w0 in range(0, CHUNK, step):
+                for s in (OWN, PREV):
+                    w1 = min(w0 + step, k_seq_rows[s] // W - c * CHUNK)
+                    row0 = b * k_seq_rows[s] + c * CHUNK * W
+                    if w1 > w0:
+                        k_view = k_rows[s][row0 + w0 * W : row0 + w1 * W, :].rearrange(
+                            "(wh a u c) d -> u c a wh d", a=P // 2, u=2, c=2
+                        )
+                        for u in range(2):
+                            for c2 in range(2):
+                                nc.sync.dma_start(
+                                    out=loaded[(s, chunk)][c2:P:2, u, 2 * w0 : 2 * w1, :], in_=k_view[u, c2]
+                                )
+                    if s == OWN:
+                        row0 = b * N + c * CHUNK * W
+                        nc.sync.dma_start(
+                            out=loaded[(QUERY, chunk)][:, w0 * QT : (w0 + step) * QT, :],
+                            in_=q_rows[row0 + w0 * W : row0 + (w0 + step) * W, :].rearrange(
+                                "(a r) d -> r a d", r=P
+                            ),
+                        )
+                row0 = b * N + c * CHUNK * W
+                nc.sync.dma_start(
+                    out=loaded[("v", chunk)][:, w0 : w0 + step, :, :],
+                    in_=v_rows[row0 + w0 * W : row0 + (w0 + step) * W, :].rearrange(
+                        "(w p j) d -> p w j d", p=P, j=4
+                    ),
                 )
-                k_raw = const.tile([P, 2, 2 * CHUNK, D], BF16, name="k_raw_%d_%d" % (s, chunk))
-                for u in range(2):
-                    for c2 in range(2):
-                        nc.sync.dma_start(out=k_raw[c2:P:2, u, 0 : 2 * windows, :], in_=k_view[u, c2])
-                loaded[(s, chunk)] = k_raw
-                if s == OWN:
-                    row0 = b * N + c * CHUNK * W
-                    q_raw = const.tile([P, CHUNK * QT, D], BF16, name="q_raw_%d" % chunk)
-                    nc.sync.dma_start(
-                        out=q_raw[:],
-                        in_=q_rows[row0 : row0 + CHUNK * W, :].rearrange("(a r) d -> r a d", r=P),
-                    )
-                    loaded[(QUERY, chunk)] = q_raw
-            row0 = b * N + c * CHUNK * W
-            v_raw = const.tile([P, CHUNK, 4, D], BF16, name="v_raw_%d" % chunk)
-            nc.sync.dma_start(
-                out=v_raw[:],
-                in_=v_rows[row0 : row0 + CHUNK * W, :].rearrange("(w p j) d -> p w j d", p=P, j=4),
-            )
-            loaded[("v", chunk)] = v_raw
 
         def parts_of(g):
             return [OWN] if g % NW == 0 else [PREV, OWN]
@@ -136,7 +144,10 @@ def tile_localattention_pa_t_kernel(tc, q_rot, k_own, k_prev, v, out):
             u, h = divmod(j, 2)
             if j == 0:
                 turned[gn] = turned_pool.tile([P, 3, W], BF16, name="turned")
-            t_ps = psum_t.tile([P, 3, P], BF16)
+            if n < 0:
+                t_ps = psum_s.tile([P, 3, P], BF16, name="s_ps")
+            else:
+                t_ps = psum_t.tile([P, 3, P], BF16, name="t_ps")
             for s in parts_of(gn):
                 w = t - 1 + s
                 k_raw = loaded[(s, b * CHUNKS + w // CHUNK)]
@@ -217,32 +228,26 @@ def tile_localattention_pa_t_kernel(tc, q_rot, k_own, k_prev, v, out):
                 in_=live[("s_ps", s, n)][:, :, 0 : columns(s, i)],
                 axis=AXIS.XY,
                 op=ALU.max,
+                negate=True,
             )
 
         def negate_max(n):
             if not 0 <= n < TILES:
                 return
             rowmax = live[("rowmax", n)]
-            negmax = small.tile([P, 1], F32)
             if len(parts_of(n // QT)) == 2:
+                negmax = small.tile([P, 1], F32)
                 nc.gpsimd.tensor_scalar(
                     out=negmax[:],
                     in0=rowmax[:, PREV : PREV + 1],
                     scalar1=rowmax[:, OWN : OWN + 1],
-                    scalar2=-1.0,
-                    op0=ALU.max,
-                    op1=ALU.mult,
+                    scalar2=LOWEST,
+                    op0=ALU.min,
+                    op1=ALU.max,
                 )
+                live[("negmax", n)] = negmax[:]
             else:
-                nc.gpsimd.tensor_scalar(
-                    out=negmax[:],
-                    in0=rowmax[:, OWN : OWN + 1],
-                    scalar1=-1.0,
-                    scalar2=0.0,
-                    op0=ALU.mult,
-                    op1=ALU.add,
-                )
-            live[("negmax", n)] = negmax
+                live[("negmax", n)] = rowmax[:, OWN : OWN + 1]
 
         def exponentials(n):
             if not 0 <= n < TILES:
@@ -257,7 +262,7 @@ def tile_localattention_pa_t_kernel(tc, q_rot, k_own, k_prev, v, out):
                     out=e_view[:, s, :, 0:cols],
                     in_=live[("s_ps", s, n)][:, :, 0:cols],
                     func=ACT.Exp,
-                    bias=live[("negmax", n)][:],
+                    bias=live[("negmax", n)],
                     scale=1.0,
                     accum_out=rowsums[g][:, i, s : s + 1],
                 )

@@ -23,7 +23,7 @@ NEG = -1.0e30
 LOWEST = -3.0e38
 CHUNK = 2
 CHUNKS = NW // CHUNK
-LOAD_AHEAD = 2
+LOAD_AHEAD = 3
 E_SLOTS = 2
 S_BANKS = 5
 

@@ -5,6 +5,7 @@ from concourse.masks import make_identity
 
 BF16 = mybir.dt.bfloat16
 F32 = mybir.dt.float32
+I32 = mybir.dt.int32
 U32 = mybir.dt.uint32
 U8 = mybir.dt.uint8
 FP8X4 = mybir.dt.float8_e4m3fn_x4
@@ -16,16 +17,40 @@ B, N, W, D = 2, 8192, 512, 128
 P = 128
 NW = N // W
 QT = W // P
-TILES = B * NW * QT
 HALF = W // 2
+DIAG = P // 2
 PREV, OWN, QUERY = 0, 1, 2
 NEG = -1.0e30
 LOWEST = -3.0e38
 CHUNK = 2
 CHUNKS = NW // CHUNK
-LOAD_AHEAD = 3
-E_SLOTS = 2
-S_BANKS = 5
+LOAD_AHEAD = 2
+V_WORDS = D + D // 4
+PART_SLOTS = 3
+
+UNITS = (((0, 0), (0, 2)), ((1, 0), (1, 2)), ((0, 1), (1, 1)), ((0, 3),), ((1, 3),))
+OWN_COLUMNS = {
+    (0, 2): (0, 192),
+    (1, 2): (0, 192),
+    (0, 0): (192, 256),
+    (1, 0): (192, 256),
+    (0, 1): (0, 128),
+    (1, 1): (128, 256),
+    (0, 3): (0, 256),
+    (1, 3): (0, 256),
+}
+GROUPS = ((0, 1), (2, 3, 4))
+BANKS = 8
+SCORES_AHEAD, MAX_AHEAD = 2, 2
+TRANSPOSE_LAG, REGROUP_LAG, QUANTISE_LAG, MULTIPLY_LAG, DIVIDE_LAG = 2, 2, 5, 6, 8
+PIECES = (
+    (OWN, 0, "scalar"),
+    (QUERY, 0, "scalar"),
+    (PREV, 0, "vector"),
+    (OWN, 1, "vector"),
+    (QUERY, 1, "scalar"),
+    (PREV, 1, "vector"),
+)
 
 FLOPS = 2 * 2 * B * (W * W + (NW - 1) * W * 2 * W) * D
 
@@ -38,15 +63,37 @@ def tile_localattention_pa_t_kernel(tc, q_rot, k_own, k_prev, v, out):
     v_rows = v.flatten_outer_dims()
     out_rows = out.flatten_outer_dims()
 
+    slots = []
+    first_slot = []
+    exp_item = {}
+    for t in range(NW):
+        first_slot.append(len(slots))
+        for unit in range(len(UNITS)):
+            own_slot = len(slots)
+            slots.append((OWN, t, unit, UNITS[unit]))
+            if t > 0:
+                for tile in UNITS[unit]:
+                    exp_item[len(slots)] = len(slots)
+                    slots.append((PREV, t, unit, (tile,)))
+            exp_item[len(slots)] = own_slot
+    first_slot.append(len(slots))
+    rounds = len(slots)
+    exp_round = {slot: k for k, slot in exp_item.items()}
+
     with ExitStack() as ctx:
         const = ctx.enter_context(tc.tile_pool(name="const", bufs=1))
-        turned_pool = ctx.enter_context(tc.tile_pool(name="turned_pool", bufs=3))
-        work = ctx.enter_context(tc.tile_pool(name="work", bufs=3))
-        small = ctx.enter_context(tc.tile_pool(name="small", bufs=6))
-        psum_s = ctx.enter_context(tc.psum_pool(name="psum_s", bufs=S_BANKS))
-        psum_e = ctx.enter_context(tc.psum_pool(name="psum_e", bufs=1))
-        psum_t = ctx.enter_context(tc.psum_pool(name="psum_t", bufs=1))
-        psum_o = ctx.enter_context(tc.psum_pool(name="psum_o", bufs=1))
+        turned_pool = ctx.enter_context(tc.tile_pool(name="turned_pool", bufs=2))
+        work = ctx.enter_context(tc.tile_pool(name="work", bufs=4))
+        codes_pool = ctx.enter_context(tc.tile_pool(name="codes_pool", bufs=10))
+        small = ctx.enter_context(tc.tile_pool(name="small", bufs=14))
+        psum = ctx.enter_context(tc.psum_pool(name="psum", bufs=1))
+        free_from = [-100.0] * BANKS
+
+        def bank_tile(shape, dtype, last_read):
+            bank = free_from.index(min(free_from))
+            free_from[bank] = last_read
+            return psum.tile(shape, dtype, name="bank_%d" % bank)
+
 
         ident_bf = const.tile([P, P], BF16)
         make_identity(nc, ident_bf[:])
@@ -62,7 +109,7 @@ def tile_localattention_pa_t_kernel(tc, q_rot, k_own, k_prev, v, out):
             pattern=[[-1, P]],
             channel_multiplier=1,
         )
-        mask_bf = const.tile([P, 2, P // 2], BF16)
+        mask_bf = const.tile([P, 2, DIAG], BF16)
         nc.vector.tensor_copy(
             out=mask_bf[:].rearrange("r u (p c) -> r u p c", c=2),
             in_=mask_f32[:].rearrange("r (p u c) -> r u p c", u=2, c=2),
@@ -70,313 +117,394 @@ def tile_localattention_pa_t_kernel(tc, q_rot, k_own, k_prev, v, out):
         ident_f32 = const.tile([P, P], F32)
         make_identity(nc, ident_f32[:])
 
-        e_tiles = [
-            [const.tile([P, 2 * W], BF16, name="e_%d_%d" % (slot, i)) for i in range(QT)]
-            for slot in range(E_SLOTS)
-        ]
-        for slot in range(E_SLOTS):
-            for i in range(QT - 1):
-                e_view = e_tiles[slot][i][:].rearrange("q (s u c) -> q s u c", s=2, u=2)
-                nc.vector.memset(e_view[:, OWN, :, (P // 2) * (i + 1) :], 0.0)
+        warm = const.tile([P, 1], F32)
+        nc.vector.memset(warm[:], 0.0)
+        warm_out = const.tile([P, 1], F32)
+        nc.scalar.activation(out=warm_out[:], in_=warm[:], func=ACT.Exp)
 
-        v_codes = const.tile([P, B * NW, D], U32, align_bytes=64)
-        v_scales = const.tile([P, B * NW, D], U8, align_bytes=64)
+        v_full = const.tile([P, B * NW, V_WORDS], I32, align_bytes=64)
+        nc.gpsimd.memset(v_full[:, :, D:], 0)
+        v_part = const.tile([P, PART_SLOTS * B * 3, V_WORDS], I32, align_bytes=64)
+        nc.vector.memset(v_part[:], 0)
+
+        def full_index(b, t):
+            return b * NW + t
+
+        def part_index(b, i, t):
+            return ((t % PART_SLOTS) * B + b) * 3 + i
+
+        def codes_of(words):
+            return words[:, 0:D].bitcast(FP8X4)
+
+        def scales_of(words):
+            return words[:, D:].bitcast(U8)
 
         loaded = {}
 
-        def load_chunk(chunk):
-            if chunk >= B * CHUNKS:
+        def chunk_tile(kind, b, c):
+            if (kind, b, c) not in loaded:
+                if kind == QUERY:
+                    loaded[(kind, b, c)] = const.tile([P, CHUNK * QT, D], BF16, name="q_raw_%d_%d" % (b, c))
+                elif kind == "v":
+                    loaded[(kind, b, c)] = const.tile([P, CHUNK, 4, D], BF16, name="v_raw_%d_%d" % (b, c))
+                else:
+                    loaded[(kind, b, c)] = const.tile(
+                        [P, 2, 2 * CHUNK, D], BF16, name="k_raw_%d_%d_%d" % (kind, b, c)
+                    )
+            return loaded[(kind, b, c)]
+
+        def load(kind, b, c, w0, w1):
+            dst = chunk_tile(kind, b, c)
+            if kind in (OWN, PREV):
+                w1 = min(w1, k_seq_rows[kind] // W - c * CHUNK)
+                row0 = b * k_seq_rows[kind] + c * CHUNK * W
+                if w1 > w0:
+                    k_view = k_rows[kind][row0 + w0 * W : row0 + w1 * W, :].rearrange(
+                        "(wh a u c) d -> u c a wh d", a=P // 2, u=2, c=2
+                    )
+                    for u in range(2):
+                        for c2 in range(2):
+                            nc.sync.dma_start(out=dst[c2:P:2, u, 2 * w0 : 2 * w1, :], in_=k_view[u, c2])
                 return
-            b, c = divmod(chunk, CHUNKS)
-            for s in (OWN, PREV):
-                loaded[(s, chunk)] = const.tile([P, 2, 2 * CHUNK, D], BF16, name="k_raw_%d_%d" % (s, chunk))
-            loaded[(QUERY, chunk)] = const.tile([P, CHUNK * QT, D], BF16, name="q_raw_%d" % chunk)
-            loaded[("v", chunk)] = const.tile([P, CHUNK, 4, D], BF16, name="v_raw_%d" % chunk)
-            step = 1 if chunk == 0 else CHUNK
-            for w0 in range(0, CHUNK, step):
-                for s in (OWN, PREV):
-                    w1 = min(w0 + step, k_seq_rows[s] // W - c * CHUNK)
-                    row0 = b * k_seq_rows[s] + c * CHUNK * W
-                    if w1 > w0:
-                        k_view = k_rows[s][row0 + w0 * W : row0 + w1 * W, :].rearrange(
-                            "(wh a u c) d -> u c a wh d", a=P // 2, u=2, c=2
-                        )
-                        for u in range(2):
-                            for c2 in range(2):
-                                nc.sync.dma_start(
-                                    out=loaded[(s, chunk)][c2:P:2, u, 2 * w0 : 2 * w1, :], in_=k_view[u, c2]
-                                )
-                    if s == OWN:
-                        row0 = b * N + c * CHUNK * W
-                        nc.sync.dma_start(
-                            out=loaded[(QUERY, chunk)][:, w0 * QT : (w0 + step) * QT, :],
-                            in_=q_rows[row0 + w0 * W : row0 + (w0 + step) * W, :].rearrange(
-                                "(a r) d -> r a d", r=P
-                            ),
-                        )
-                row0 = b * N + c * CHUNK * W
+            row0 = b * N + c * CHUNK * W
+            if kind == QUERY:
                 nc.sync.dma_start(
-                    out=loaded[("v", chunk)][:, w0 : w0 + step, :, :],
-                    in_=v_rows[row0 + w0 * W : row0 + (w0 + step) * W, :].rearrange(
-                        "(w p j) d -> p w j d", p=P, j=4
-                    ),
+                    out=dst[:, w0 * QT : w1 * QT, :],
+                    in_=q_rows[row0 + w0 * W : row0 + w1 * W, :].rearrange("(a r) d -> r a d", r=P),
+                )
+            else:
+                nc.sync.dma_start(
+                    out=dst[:, w0:w1, :, :],
+                    in_=v_rows[row0 + w0 * W : row0 + w1 * W, :].rearrange("(w p j) d -> p w j d", p=P, j=4),
                 )
 
-        def parts_of(g):
-            return [OWN] if g % NW == 0 else [PREV, OWN]
+        def load_chunk(c):
+            if c >= CHUNKS:
+                return
+            for b in range(B):
+                for kind in (OWN, QUERY, PREV):
+                    load(kind, b, c, 0, CHUNK)
+            for b in range(B):
+                load("v", b, c, 0, CHUNK)
 
-        def columns(s, i):
-            return HALF if s == PREV else (P // 2) * (i + 1)
+        def load_first_chunk():
+            for b in range(B):
+                load(OWN, b, 0, 0, 1)
+                load(QUERY, b, 0, 0, 1)
+            for b in range(B):
+                load("v", b, 0, 0, 1)
+            for b in range(B):
+                load(OWN, b, 0, 1, 2)
+                load(QUERY, b, 0, 1, 2)
+                load(PREV, b, 0, 0, 2)
+            for b in range(B):
+                load("v", b, 0, 1, 2)
 
         turned = {}
-        rowsums = {}
-        recips = {}
-        outputs = {}
         live = {}
 
-        def prepare_transposes(n):
-            gn, j = n // QT + 1, n % QT
-            if not 0 <= gn < B * NW:
-                return
-            if j == 0 and gn % CHUNK == 0:
-                load_chunk(gn // CHUNK + LOAD_AHEAD)
-            b, t = divmod(gn, NW)
-            u, h = divmod(j, 2)
-            if j == 0:
-                turned[gn] = turned_pool.tile([P, 3, W], BF16, name="turned")
-            if n < 0:
-                t_ps = psum_s.tile([P, 3, P], BF16, name="s_ps")
-            else:
-                t_ps = psum_t.tile([P, 3, P], BF16, name="t_ps")
-            for s in parts_of(gn):
-                w = t - 1 + s
-                k_raw = loaded[(s, b * CHUNKS + w // CHUNK)]
-                nc.tensor.transpose(t_ps[:, s, :], k_raw[:, u, 2 * (w % CHUNK) + h, :], ident_bf[:])
-            q_raw = loaded[(QUERY, gn // CHUNK)]
-            nc.tensor.transpose(t_ps[:, QUERY, :], q_raw[:, (gn % CHUNK) * QT + j, :], ident_bf[:])
-            live[("t_ps", n)] = t_ps
+        def prepare_transposes(kind, b, t, k):
+            w = t - 1 if kind == PREV else t
+            raw = chunk_tile(kind, b, w // CHUNK)
+            t_ps = bank_tile([P, W], BF16, k + 0.5)
+            for j in range(QT):
+                if kind == QUERY:
+                    rows = raw[:, (w % CHUNK) * QT + j, :]
+                else:
+                    rows = raw[:, j // 2, 2 * (w % CHUNK) + j % 2, :]
+                nc.tensor.transpose(t_ps[:, j * P : (j + 1) * P], rows, ident_bf[:])
+            live[("t_ps", kind, b, t)] = t_ps
 
-        def prepare_copy(n, engine):
-            gn, j = n // QT + 1, n % QT
-            if not 0 <= gn < B * NW or (j == 0) != (engine == "scalar"):
-                return
-            first = parts_of(gn)[0]
-            quarter = turned[gn][:, first:, j * P : (j + 1) * P]
+        def prepare_copy(kind, b, t, engine):
+            t_sb = turned_pool.tile([P, W], BF16, name="turned_%d_%d" % (kind, b))
+            turned[(kind, b, t)] = t_sb
+            t_ps = live[("t_ps", kind, b, t)]
             if engine == "scalar":
-                nc.scalar.copy(out=quarter, in_=live[("t_ps", n)][:, first:, :])
+                nc.scalar.copy(out=t_sb[:].bitcast(F32), in_=t_ps[:].bitcast(F32))
             else:
-                nc.vector.tensor_copy(out=quarter, in_=live[("t_ps", n)][:, first:, :])
+                nc.vector.tensor_copy(out=t_sb[:].bitcast(F32), in_=t_ps[:].bitcast(F32))
 
-        def interleave_v(n):
-            gn, j = n // QT + 1, n % QT
-            if not 0 <= gn < B * NW:
-                return
-            if j == 0:
-                live[("v_grouped", gn)] = work.tile([P, D, 4], BF16, align_bytes=64, name="v_grouped")
-            v_raw = loaded[("v", gn // CHUNK)]
-            features = slice(j * (D // QT), (j + 1) * (D // QT))
+        def interleave_v(b, t, quarter):
+            if quarter == 0:
+                live[("v_grouped", b, t)] = work.tile([P, D, 4], BF16, align_bytes=64, name="v_grouped")
+            v_raw = chunk_tile("v", b, t // CHUNK)
+            features = slice(quarter * (D // 4), (quarter + 1) * (D // 4))
             nc.gpsimd.tensor_scalar(
-                out=live[("v_grouped", gn)][:, features, :],
-                in0=v_raw[:, gn % CHUNK, :, features].rearrange("p j d -> p d j"),
+                out=live[("v_grouped", b, t)][:, features, :],
+                in0=v_raw[:, t % CHUNK, :, features].rearrange("p j d -> p d j"),
                 scalar1=1.0,
                 scalar2=0.0,
                 op0=ALU.mult,
                 op1=ALU.add,
             )
 
-        def quantise_v(n):
-            gn, j = n // QT, n % QT
-            if not 0 <= gn < B * NW or j != 0:
-                return
+        def quantise_v(b, t):
+            words = v_full[:, full_index(b, t), :]
             nc.vector.quantize_mx(
-                out=v_codes[:, gn, :].bitcast(FP8X4),
-                scales=v_scales[:, gn, :],
-                in_=live[("v_grouped", gn)][:].rearrange("p d j -> p (d j)"),
+                out=codes_of(words),
+                scales=scales_of(words),
+                in_=live[("v_grouped", b, t)][:].rearrange("p d j -> p (d j)"),
             )
 
-        def scores(n, s):
-            g, i = divmod(n, QT)
-            if not 0 <= n < TILES or s not in parts_of(g):
-                return
-            cols = columns(s, i)
-            s_ps = psum_s.tile([P, 2, HALF], F32)
-            nc.tensor.matmul(
-                s_ps[:, :, 0:cols],
-                lhsT=turned[g][:, QUERY, i * P : (i + 1) * P],
-                rhs=turned[g][:, s, :].rearrange("d (u c) -> d u c", u=2)[:, :, 0:cols],
-                start=True,
-                stop=(s == PREV),
-            )
-            if s == OWN:
+        def move_v(b, t):
+            for i in range(3):
+                c0, c1 = OWN_COLUMNS[(b, i)]
+                nc.sync.dma_start(
+                    out=v_part[c0 // 2 : c1 // 2, part_index(b, i, t), :],
+                    in_=v_full[0 : (c1 - c0) // 2, full_index(b, t), :],
+                )
+
+        def scores(slot):
+            kind, t, unit, tiles = slots[slot]
+            s_ps = bank_tile([P, 2, HALF], F32, exp_round[slot] + 0.4)
+            for b, i in tiles:
+                c0, c1 = (0, HALF) if kind == PREV else OWN_COLUMNS[(b, i)]
                 nc.tensor.matmul(
-                    s_ps[:, :, cols - P // 2 : cols],
-                    lhsT=ident_bf[:],
-                    rhs=mask_bf[:],
-                    start=False,
-                    stop=True,
+                    s_ps[:, :, c0:c1],
+                    lhsT=turned[(QUERY, b, t)][:, i * P : (i + 1) * P],
+                    rhs=turned[(kind, b, t)][:].rearrange("d (u c) -> d u c", u=2)[:, :, 0 : c1 - c0],
+                    start=True,
+                    stop=(kind == PREV),
                 )
-            live[("s_ps", s, n)] = s_ps
+                if kind == OWN:
+                    nc.tensor.matmul(
+                        s_ps[:, :, c1 - DIAG : c1],
+                        lhsT=ident_bf[:],
+                        rhs=mask_bf[:],
+                        start=False,
+                        stop=True,
+                    )
+            live[("s_ps", slot)] = s_ps
 
-        def row_max(n, s):
-            g, i = divmod(n, QT)
-            if not 0 <= n < TILES or s not in parts_of(g):
-                return
-            if s == parts_of(g)[0]:
-                live[("rowmax", n)] = small.tile([P, 2], F32, name="rowmax")
-            nc.vector.tensor_reduce(
-                out=live[("rowmax", n)][:, s : s + 1],
-                in_=live[("s_ps", s, n)][:, :, 0 : columns(s, i)],
-                axis=AXIS.XY,
-                op=ALU.max,
-                negate=True,
-            )
-
-        def negate_max(n):
-            if not 0 <= n < TILES:
-                return
-            rowmax = live[("rowmax", n)]
-            if len(parts_of(n // QT)) == 2:
-                negmax = small.tile([P, 1], F32)
-                nc.gpsimd.tensor_scalar(
-                    out=negmax[:],
-                    in0=rowmax[:, PREV : PREV + 1],
-                    scalar1=rowmax[:, OWN : OWN + 1],
-                    scalar2=LOWEST,
-                    op0=ALU.min,
-                    op1=ALU.max,
+        def row_max(slot):
+            kind, t, unit, tiles = slots[slot]
+            for b, i in tiles:
+                c0, c1 = (0, HALF) if kind == PREV else OWN_COLUMNS[(b, i)]
+                if kind == OWN:
+                    live[("rowmax", t, b, i)] = small.tile([P, 2], F32, name="rowmax")
+                nc.vector.tensor_reduce(
+                    out=live[("rowmax", t, b, i)][:, kind : kind + 1],
+                    in_=live[("s_ps", slot)][:, :, c0:c1],
+                    axis=AXIS.XY,
+                    op=ALU.max,
+                    negate=True,
                 )
-                live[("negmax", n)] = negmax[:]
-            else:
-                live[("negmax", n)] = rowmax[:, OWN : OWN + 1]
 
-        def exponentials(n):
-            if not 0 <= n < TILES:
-                return
-            g, i = divmod(n, QT)
-            if i == 0:
-                rowsums[g] = small.tile([P, QT, 2], F32, name="rowsum")
-            e_view = e_tiles[g % E_SLOTS][i][:].rearrange("q (s u c) -> q s u c", s=2, u=2)
-            for s in parts_of(g):
-                cols = columns(s, i)
+        def negate_max(slot):
+            kind, t, unit, tiles = slots[slot]
+            for b, i in tiles:
+                rowmax = live[("rowmax", t, b, i)]
+                if t == 0:
+                    live[("negmax", t, b, i)] = rowmax[:, OWN : OWN + 1]
+                elif kind == PREV:
+                    negmax = small.tile([P, 1], F32, name="negmax")
+                    nc.gpsimd.tensor_scalar(
+                        out=negmax[:],
+                        in0=rowmax[:, PREV : PREV + 1],
+                        scalar1=rowmax[:, OWN : OWN + 1],
+                        scalar2=LOWEST,
+                        op0=ALU.min,
+                        op1=ALU.max,
+                    )
+                    live[("negmax", t, b, i)] = negmax[:]
+
+        group_of = {}
+        group_tiles = []
+        for group in range(len(GROUPS)):
+            members = [tile for unit in GROUPS[group] for tile in UNITS[unit]]
+            group_tiles.append(members)
+            for place in range(len(members)):
+                group_of[members[place]] = (group, place)
+
+        def exponentials(k):
+            slot = exp_item[k]
+            kind, t, unit, tiles = slots[slot]
+            half = (k - 1) % 2
+            pair = (k - 1) // 2
+            if half == 0:
+                live[("e", pair)] = work.tile([P, 2, 2, HALF], BF16, align_bytes=64, name="e")
+            for b, i in tiles:
+                group, place = group_of[(b, i)]
+                if ("rowsum", t, group) not in live:
+                    live[("rowsum", t, group)] = small.tile([P, QT, 2], F32, name="rowsum")
+                c0, c1 = (0, HALF) if kind == PREV else OWN_COLUMNS[(b, i)]
                 nc.scalar.activation(
-                    out=e_view[:, s, :, 0:cols],
-                    in_=live[("s_ps", s, n)][:, :, 0:cols],
+                    out=live[("e", pair)][:, half, :, c0:c1],
+                    in_=live[("s_ps", slot)][:, :, c0:c1],
                     func=ACT.Exp,
-                    bias=live[("negmax", n)],
+                    bias=live[("negmax", t, b, i)],
                     scale=1.0,
-                    accum_out=rowsums[g][:, i, s : s + 1],
+                    accum_out=live[("rowsum", t, group)][:, place, kind : kind + 1],
                 )
 
-        def transpose_e(n):
-            if not 0 <= n < TILES:
-                return
-            g, i = divmod(n, QT)
-            e_words = e_tiles[g % E_SLOTS][i][:].bitcast(F32)
-            eT_ps = psum_e.tile([P, 2, 2, P], F32)
-            for s in parts_of(g):
+        def transpose_e(pair):
+            e_words = live[("e", pair)][:].rearrange("q h u c -> q (h u c)").bitcast(F32)
+            eT_ps = bank_tile([P, 2, 2, P], F32, 2 * pair + 2 + REGROUP_LAG + 0.9)
+            for h in range(2):
                 for u in range(2):
-                    word0 = (2 * s + u) * P
-                    nc.tensor.transpose(eT_ps[:, s, u, :], e_words[:, word0 : word0 + P], ident_f32[:])
-            live[("eT_ps", n)] = eT_ps
+                    word0 = (2 * h + u) * P
+                    nc.tensor.transpose(eT_ps[:, h, u, :], e_words[:, word0 : word0 + P], ident_f32[:])
+            live[("eT_ps", pair)] = eT_ps
 
-        def regroup_e(n):
-            if not 0 <= n < TILES:
-                return
-            first = parts_of(n // QT)[0]
-            grouped = work.tile([P, 2 * P * 4], BF16, align_bytes=64)
-            grouped_words = grouped[:].bitcast(F32).rearrange("p (s q u) -> p s q u", s=2, u=2)
+        def regroup_e(pair):
+            grouped = work.tile([P, 2 * P * 4], BF16, align_bytes=64, name="grouped")
             nc.scalar.copy(
-                out=grouped_words[:, first:, :, :],
-                in_=live[("eT_ps", n)][:, first:, :, :].rearrange("p s u q -> p s q u"),
+                out=grouped[:].bitcast(F32).rearrange("p (h q u) -> p h q u", h=2, u=2),
+                in_=live[("eT_ps", pair)][:].rearrange("p h u q -> p h q u"),
             )
-            live[("grouped", n)] = grouped
+            live[("grouped", pair)] = grouped
 
-        def quantise_e(n):
-            if not 0 <= n < TILES:
-                return
-            first = parts_of(n // QT)[0]
-            e_codes = work.tile([P, 2 * P], U32, align_bytes=64)
-            e_scales = work.tile([P, 2 * P], U8, align_bytes=64)
-            nc.vector.quantize_mx(
-                out=e_codes[:, first * P :].bitcast(FP8X4),
-                scales=e_scales[:, first * P :],
-                in_=live[("grouped", n)][:, first * P * 4 :],
-            )
-            live[("e_codes", n)] = e_codes
-            live[("e_scales", n)] = e_scales
+        def quantise_e(pair):
+            e_codes = codes_pool.tile([P, 2 * P], U32, align_bytes=64, name="e_codes")
+            e_scales = codes_pool.tile([P, 2 * P], U8, align_bytes=64, name="e_scales")
+            nc.vector.quantize_mx(out=e_codes[:].bitcast(FP8X4), scales=e_scales[:], in_=live[("grouped", pair)][:])
+            live[("e_codes", pair)] = e_codes
+            live[("e_scales", pair)] = e_scales
 
-        def multiply_v(n):
-            if not 0 <= n < TILES:
-                return
-            g, i = divmod(n, QT)
-            if i == 0:
-                outputs[g] = psum_o.tile([P, QT, D], F32, name="o_ps")
-            for s in parts_of(g):
-                nc.tensor.matmul_mx(
-                    out=outputs[g][:, i, :],
-                    lhsT=live[("e_codes", n)][:, s * P : (s + 1) * P].bitcast(FP8X4),
-                    lhsT_scale=live[("e_scales", n)][:, s * P : (s + 1) * P],
-                    rhs=v_codes[:, g - 1 + s, :].bitcast(FP8X4),
-                    rhs_scale=v_scales[:, g - 1 + s, :],
-                    start=(s == parts_of(g)[0]),
-                    stop=(s == OWN),
-                )
+        def multiply_v(t, unit):
+            for b, i in UNITS[unit]:
+                group, place = group_of[(b, i)]
+                if place == 0:
+                    live[("o_ps", t, group)] = bank_tile([P, QT, D], F32, divide_round[(t, group)] + 0.9)
+                passes = []
+                own = first_slot[t] + sum(1 + (len(UNITS[n]) if t > 0 else 0) for n in range(unit))
+                if t > 0:
+                    prev = own + 1 + UNITS[unit].index((b, i))
+                    passes.append((exp_round[prev], v_full[:, full_index(b, t - 1), :]))
+                own_words = v_full[:, full_index(b, t), :] if i == 3 else v_part[:, part_index(b, i, t), :]
+                passes.append((exp_round[own], own_words))
+                for n in range(len(passes)):
+                    k, words = passes[n]
+                    half = (k - 1) % 2
+                    pair = (k - 1) // 2
+                    nc.tensor.matmul_mx(
+                        out=live[("o_ps", t, group)][:, place, :],
+                        lhsT=live[("e_codes", pair)][:, half * P : (half + 1) * P].bitcast(FP8X4),
+                        lhsT_scale=live[("e_scales", pair)][:, half * P : (half + 1) * P],
+                        rhs=codes_of(words),
+                        rhs_scale=scales_of(words),
+                        start=(n == 0),
+                        stop=(n == len(passes) - 1),
+                    )
 
-        def sum_rows(n):
-            g, i = divmod(n, QT)
-            if not 0 <= n < TILES or i != QT - 1:
-                return
-            if len(parts_of(g)) == 2:
-                total = small.tile([P, QT], F32)
-                nc.gpsimd.tensor_tensor(
-                    out=total[:], in0=rowsums[g][:, :, PREV], in1=rowsums[g][:, :, OWN], op=ALU.add
-                )
-                live[("total", g)] = total[:]
+        def sum_rows(t, group):
+            rowsum = live[("rowsum", t, group)]
+            if t > 0:
+                total = small.tile([P, QT], F32, name="total")
+                nc.gpsimd.tensor_tensor(out=total[:], in0=rowsum[:, :, PREV], in1=rowsum[:, :, OWN], op=ALU.add)
+                live[("total", t, group)] = total[:]
             else:
-                live[("total", g)] = rowsums[g][:, :, OWN]
+                live[("total", t, group)] = rowsum[:, :, OWN]
 
-        def invert_sums(n):
-            g, i = divmod(n, QT)
-            if not 0 <= n < TILES or i != QT - 1:
-                return
-            recips[g] = small.tile([P, QT], F32, name="recip")
-            nc.vector.reciprocal(out=recips[g][:], in_=live[("total", g)])
+        def invert_sums(t, group):
+            recip = small.tile([P, QT], F32, name="recip")
+            nc.vector.reciprocal(out=recip[:], in_=live[("total", t, group)])
+            live[("recip", t, group)] = recip
 
-        def divide_and_store(n):
-            g, i = divmod(n, QT)
-            if not 0 <= n < TILES or i != QT - 1:
-                return
-            o_sb = work.tile([P, QT, D], F32)
+        def divide_and_store(t, group):
+            o_sb = work.tile([P, QT, D], F32, name="o_sb")
             nc.vector.tensor_tensor(
                 out=o_sb[:],
-                in0=outputs[g][:],
-                in1=recips[g][:].unsqueeze(2).to_broadcast([P, QT, D]),
+                in0=live[("o_ps", t, group)][:],
+                in1=live[("recip", t, group)][:].unsqueeze(2).to_broadcast([P, QT, D]),
                 op=ALU.mult,
             )
-            nc.sync.dma_start(
-                out=out_rows[g * W : (g + 1) * W, :].rearrange("(a r) d -> r a d", r=P), in_=o_sb[:]
-            )
+            for b in range(B):
+                places = [place for place in range(QT) if group_tiles[group][place][0] == b]
+                i = group_tiles[group][places[0]][1]
+                row0 = b * N + t * W
+                nc.sync.dma_start(
+                    out=out_rows[row0 : row0 + W, :].rearrange("(a r) d -> r a d", r=P)[:, i::2, :],
+                    in_=o_sb[:, places[0] : places[1] + 1 : places[1] - places[0], :],
+                )
 
-        for chunk in range(LOAD_AHEAD):
-            load_chunk(chunk)
+        divide_round = {}
+        plan = {}
+
+        def at(stage, k, args):
+            plan.setdefault((stage, k), []).append(args)
+
+        for pair in range(rounds // 2):
+            last = 2 * pair + 2
+            at("transpose_e", last + TRANSPOSE_LAG, (pair,))
+            at("regroup_e", last + REGROUP_LAG, (pair,))
+            at("quantise_e", last + QUANTISE_LAG, (pair,))
+        for t in range(NW):
+            for group in range(len(GROUPS)):
+                unit = GROUPS[group][-1]
+                own = first_slot[t] + sum(1 + (len(UNITS[n]) if t > 0 else 0) for n in range(unit))
+                pair = (exp_round[own] - 1) // 2
+                for n in range(len(GROUPS[group])):
+                    at("multiply_v", 2 * pair + 2 + MULTIPLY_LAG + n, (t, GROUPS[group][n]))
+                at("sum_rows", 2 * pair + 4, (t, group))
+                at("invert_sums", 2 * pair + 1 + DIVIDE_LAG, (t, group))
+                at("divide", 2 * pair + 2 + DIVIDE_LAG, (t, group))
+                divide_round[(t, group)] = 2 * pair + 2 + DIVIDE_LAG
+        for t in range(1, NW):
+            k0, k1 = first_slot[t - 1], first_slot[t]
+            for n in range(len(PIECES)):
+                kind, b, engine = PIECES[n]
+                at("prepare", k0 + n * (k1 - k0) // len(PIECES), (kind, b, t, engine))
+            for b in range(B):
+                for quarter in range(4):
+                    k = k0 + (4 * b + quarter) * (k1 - k0) // 8
+                    at("interleave_v", k, (b, t, quarter))
+                at("quantise_v", k + 1, (b, t))
+                at("move_v", k + 1, (b, t))
+            if t % CHUNK == 0:
+                at("load_chunk", k0, (t // CHUNK + LOAD_AHEAD,))
+        for c in range(1, LOAD_AHEAD + 1):
+            at("load_chunk", 2, (c,))
+
+        load_first_chunk()
 
         with tc.manual_schedule():
-            for k in range(-QT - 2, TILES + 4):
-                prepare_transposes(k + 2)
-                transpose_e(k - 1)
-                scores(k + 2, PREV)
-                multiply_v(k - 3)
-                scores(k + 2, OWN)
-                row_max(k + 1, PREV)
-                row_max(k + 1, OWN)
-                quantise_e(k - 2)
-                prepare_copy(k + 2, "vector")
-                quantise_v(k + 2)
-                invert_sums(k - 2)
-                divide_and_store(k - 3)
-                negate_max(k + 1)
-                sum_rows(k - 1)
-                interleave_v(k + 2)
-                exponentials(k)
-                prepare_copy(k + 2, "scalar")
-                regroup_e(k - 1)
+            for n in range(4):
+                b, kind = n // 2, (OWN, QUERY)[n % 2]
+                prepare_transposes(kind, b, 0, -SCORES_AHEAD)
+                prepare_copy(kind, b, 0, ("vector", "scalar")[n % 2])
+            for b in range(B):
+                for quarter in range(4):
+                    interleave_v(b, 0, quarter)
+            for k in range(-SCORES_AHEAD, rounds + 16):
+                if 0 <= k + SCORES_AHEAD < rounds:
+                    scores(k + SCORES_AHEAD)
+                for args in plan.get(("prepare", k), []):
+                    prepare_transposes(args[0], args[1], args[2], k)
+                for args in plan.get(("multiply_v", k), []):
+                    multiply_v(*args)
+                for args in plan.get(("transpose_e", k), []):
+                    transpose_e(*args)
+                for args in plan.get(("quantise_e", k), []):
+                    quantise_e(*args)
+                if 0 <= k + MAX_AHEAD < rounds:
+                    row_max(k + MAX_AHEAD)
+                for args in plan.get(("prepare", k), []):
+                    if args[3] == "vector":
+                        prepare_copy(*args)
+                for args in plan.get(("quantise_v", k), []):
+                    quantise_v(*args)
+                if k in (0, 1):
+                    quantise_v(k, 0)
+                    move_v(k, 0)
+                for args in plan.get(("invert_sums", k), []):
+                    invert_sums(*args)
+                for args in plan.get(("divide", k), []):
+                    divide_and_store(*args)
+                if 0 <= k + MAX_AHEAD < rounds:
+                    negate_max(k + MAX_AHEAD)
+                for args in plan.get(("sum_rows", k), []):
+                    sum_rows(*args)
+                for args in plan.get(("interleave_v", k), []):
+                    interleave_v(*args)
+                if k in exp_item:
+                    exponentials(k)
+                for args in plan.get(("prepare", k), []):
+                    if args[3] == "scalar":
+                        prepare_copy(*args)
+                for args in plan.get(("regroup_e", k), []):
+                    regroup_e(*args)
+                for args in plan.get(("move_v", k), []):
+                    move_v(*args)
+                for args in plan.get(("load_chunk", k), []):
+                    load_chunk(*args)

@@ -41,6 +41,7 @@ OWN_COLUMNS = {
 }
 GROUPS = ((0, 1), (2, 3, 4))
 BANKS = 8
+FIRST_WAIT = 1
 SCORES_AHEAD, MAX_AHEAD = 2, 2
 TRANSPOSE_LAG, REGROUP_LAG, QUANTISE_LAG, MULTIPLY_LAG, DIVIDE_LAG = 2, 2, 5, 6, 8
 PIECES = (
@@ -182,23 +183,11 @@ def tile_localattention_pa_t_kernel(tc, q_rot, k_own, k_prev, v, out):
             if c >= CHUNKS:
                 return
             for b in range(B):
-                for kind in (OWN, QUERY, PREV):
+                load(OWN, b, c, 0, CHUNK)
+                load(QUERY, b, c, 0, CHUNK)
+            for kind in ("v", PREV):
+                for b in range(B):
                     load(kind, b, c, 0, CHUNK)
-            for b in range(B):
-                load("v", b, c, 0, CHUNK)
-
-        def load_first_chunk():
-            for b in range(B):
-                load(OWN, b, 0, 0, 1)
-                load(QUERY, b, 0, 0, 1)
-            for b in range(B):
-                load("v", b, 0, 0, 1)
-            for b in range(B):
-                load(OWN, b, 0, 1, 2)
-                load(QUERY, b, 0, 1, 2)
-                load(PREV, b, 0, 0, 2)
-            for b in range(B):
-                load("v", b, 0, 1, 2)
 
         turned = {}
         live = {}
@@ -278,13 +267,25 @@ def tile_localattention_pa_t_kernel(tc, q_rot, k_own, k_prev, v, out):
 
         def row_max(slot):
             kind, t, unit, tiles = slots[slot]
-            for b, i in tiles:
-                c0, c1 = (0, HALF) if kind == PREV else OWN_COLUMNS[(b, i)]
-                if kind == OWN:
-                    live[("rowmax", t, b, i)] = small.tile([P, 2], F32, name="rowmax")
+            maxima = small.tile([P, 2], F32, name="own_max" if kind == OWN else "prev_max")
+            columns = [(0, HALF) if kind == PREV else OWN_COLUMNS[tile] for tile in tiles]
+            s_ps = live[("s_ps", slot)]
+            for n in range(len(tiles)):
+                live[("max", kind, t, tiles[n])] = maxima[:, n : n + 1]
+            if len(tiles) == 2 and columns[0][1] == HALF // 2:
                 nc.vector.tensor_reduce(
-                    out=live[("rowmax", t, b, i)][:, kind : kind + 1],
-                    in_=live[("s_ps", slot)][:, :, c0:c1],
+                    out=maxima[:],
+                    in_=s_ps[:].rearrange("q u (n c) -> q n u c", n=2),
+                    axis=AXIS.XY,
+                    op=ALU.max,
+                    negate=True,
+                )
+                return
+            for n in range(len(tiles)):
+                c0, c1 = columns[n]
+                nc.vector.tensor_reduce(
+                    out=maxima[:, n : n + 1],
+                    in_=s_ps[:, :, c0:c1],
                     axis=AXIS.XY,
                     op=ALU.max,
                     negate=True,
@@ -293,15 +294,14 @@ def tile_localattention_pa_t_kernel(tc, q_rot, k_own, k_prev, v, out):
         def negate_max(slot):
             kind, t, unit, tiles = slots[slot]
             for b, i in tiles:
-                rowmax = live[("rowmax", t, b, i)]
                 if t == 0:
-                    live[("negmax", t, b, i)] = rowmax[:, OWN : OWN + 1]
+                    live[("negmax", t, b, i)] = live[("max", OWN, t, (b, i))]
                 elif kind == PREV:
                     negmax = small.tile([P, 1], F32, name="negmax")
                     nc.gpsimd.tensor_scalar(
                         out=negmax[:],
-                        in0=rowmax[:, PREV : PREV + 1],
-                        scalar1=rowmax[:, OWN : OWN + 1],
+                        in0=live[("max", PREV, t, (b, i))],
+                        scalar1=live[("max", OWN, t, (b, i))],
                         scalar2=LOWEST,
                         op0=ALU.min,
                         op1=ALU.max,
@@ -433,7 +433,7 @@ def tile_localattention_pa_t_kernel(tc, q_rot, k_own, k_prev, v, out):
             for group in range(len(GROUPS)):
                 unit = GROUPS[group][-1]
                 own = first_slot[t] + sum(1 + (len(UNITS[n]) if t > 0 else 0) for n in range(unit))
-                pair = (exp_round[own] - 1) // 2
+                pair = (exp_round[own] - 1) // 2 + (FIRST_WAIT if t == 0 else 0)
                 for n in range(len(GROUPS[group])):
                     at("multiply_v", 2 * pair + 2 + MULTIPLY_LAG + n, (t, GROUPS[group][n]))
                 at("sum_rows", 2 * pair + 4, (t, group))
@@ -453,21 +453,25 @@ def tile_localattention_pa_t_kernel(tc, q_rot, k_own, k_prev, v, out):
                 at("move_v", k + 1, (b, t))
             if t % CHUNK == 0:
                 at("load_chunk", k0, (t // CHUNK + LOAD_AHEAD,))
-        for c in range(1, LOAD_AHEAD + 1):
-            at("load_chunk", 2, (c,))
+        at("load_chunk", 6, (LOAD_AHEAD,))
 
-        load_first_chunk()
+        for c in range(LOAD_AHEAD):
+            load_chunk(c)
 
         with tc.manual_schedule():
-            for n in range(4):
-                b, kind = n // 2, (OWN, QUERY)[n % 2]
-                prepare_transposes(kind, b, 0, -SCORES_AHEAD)
-                prepare_copy(kind, b, 0, ("vector", "scalar")[n % 2])
+            for b in range(B):
+                for kind, engine in ((OWN, "vector"), (QUERY, "scalar")):
+                    prepare_transposes(kind, b, 0, -SCORES_AHEAD)
+                    prepare_copy(kind, b, 0, engine)
+                if b == 0:
+                    scores(0)
+                    row_max(0)
+                    negate_max(0)
             for b in range(B):
                 for quarter in range(4):
                     interleave_v(b, 0, quarter)
             for k in range(-SCORES_AHEAD, rounds + 16):
-                if 0 <= k + SCORES_AHEAD < rounds:
+                if 0 < k + SCORES_AHEAD < rounds:
                     scores(k + SCORES_AHEAD)
                 for args in plan.get(("prepare", k), []):
                     prepare_transposes(args[0], args[1], args[2], k)
@@ -477,7 +481,7 @@ def tile_localattention_pa_t_kernel(tc, q_rot, k_own, k_prev, v, out):
                     transpose_e(*args)
                 for args in plan.get(("quantise_e", k), []):
                     quantise_e(*args)
-                if 0 <= k + MAX_AHEAD < rounds:
+                if 0 < k + MAX_AHEAD < rounds:
                     row_max(k + MAX_AHEAD)
                 for args in plan.get(("prepare", k), []):
                     if args[3] == "vector":
@@ -491,7 +495,7 @@ def tile_localattention_pa_t_kernel(tc, q_rot, k_own, k_prev, v, out):
                     invert_sums(*args)
                 for args in plan.get(("divide", k), []):
                     divide_and_store(*args)
-                if 0 <= k + MAX_AHEAD < rounds:
+                if 0 < k + MAX_AHEAD < rounds:
                     negate_max(k + MAX_AHEAD)
                 for args in plan.get(("sum_rows", k), []):
                     sum_rows(*args)

@@ -17,8 +17,7 @@ B, N, W, D = 2, 8192, 512, 128
 P = 128
 NW = N // W
 QT = W // P
-HALF = W // 2
-DIAG = P // 2
+DIAG = P // 4
 PREV, OWN, QUERY = 0, 1, 2
 NEG = -1.0e30
 LOWEST = -3.0e38
@@ -29,15 +28,15 @@ V_WORDS = D + D // 4
 PART_SLOTS = 3
 
 UNITS = (((0, 0), (0, 2)), ((1, 0), (1, 2)), ((0, 1), (1, 1)), ((0, 3),), ((1, 3),))
-OWN_COLUMNS = {
-    (0, 2): (0, 192),
-    (1, 2): (0, 192),
-    (0, 0): (192, 256),
-    (1, 0): (192, 256),
-    (0, 1): (0, 128),
-    (1, 1): (128, 256),
-    (0, 3): (0, 256),
-    (1, 3): (0, 256),
+OWN_PARTITIONS = {
+    (0, 2): (0, 96),
+    (1, 2): (0, 96),
+    (0, 0): (96, 128),
+    (1, 0): (96, 128),
+    (0, 1): (0, 64),
+    (1, 1): (64, 128),
+    (0, 3): (0, 128),
+    (1, 3): (0, 128),
 }
 GROUPS = ((0, 1), (2, 3, 4))
 BANKS = 8
@@ -59,9 +58,12 @@ FLOPS = 2 * 2 * B * (W * W + (NW - 1) * W * 2 * W) * D
 def tile_localattention_pa_t_kernel(tc, q_rot, k_own, k_prev, v, out):
     nc = tc.nc
     q_rows = q_rot.flatten_outer_dims()
-    k_rows = {OWN: k_own.flatten_outer_dims(), PREV: k_prev.flatten_outer_dims()}
-    k_seq_rows = {OWN: N, PREV: N - W}
-    v_rows = v.flatten_outer_dims()
+    key_rows = {
+        OWN: k_own.flatten_outer_dims(),
+        PREV: k_prev.flatten_outer_dims(),
+        "v": v.flatten_outer_dims(),
+    }
+    seq_rows = {OWN: N, PREV: N - W, "v": N}
     out_rows = out.flatten_outer_dims()
 
     slots = []
@@ -110,10 +112,10 @@ def tile_localattention_pa_t_kernel(tc, q_rot, k_own, k_prev, v, out):
             pattern=[[-1, P]],
             channel_multiplier=1,
         )
-        mask_bf = const.tile([P, 2, DIAG], BF16)
+        mask_bf = const.tile([P, 4, DIAG], BF16)
         nc.vector.tensor_copy(
-            out=mask_bf[:].rearrange("r u (p c) -> r u p c", c=2),
-            in_=mask_f32[:].rearrange("r (p u c) -> r u p c", u=2, c=2),
+            out=mask_bf[:],
+            in_=mask_f32[:].rearrange("r (p j) -> r j p", j=4),
         )
         ident_f32 = const.tile([P, P], F32)
         make_identity(nc, ident_f32[:])
@@ -146,48 +148,41 @@ def tile_localattention_pa_t_kernel(tc, q_rot, k_own, k_prev, v, out):
             if (kind, b, c) not in loaded:
                 if kind == QUERY:
                     loaded[(kind, b, c)] = const.tile([P, CHUNK * QT, D], BF16, name="q_raw_%d_%d" % (b, c))
-                elif kind == "v":
-                    loaded[(kind, b, c)] = const.tile([P, CHUNK, 4, D], BF16, name="v_raw_%d_%d" % (b, c))
                 else:
-                    loaded[(kind, b, c)] = const.tile(
-                        [P, 2, 2 * CHUNK, D], BF16, name="k_raw_%d_%d_%d" % (kind, b, c)
-                    )
+                    loaded[(kind, b, c)] = const.tile([P, CHUNK, 4, D], BF16, name="rows_%s_%d_%d" % (kind, b, c))
             return loaded[(kind, b, c)]
 
         def load(kind, b, c, w0, w1):
             dst = chunk_tile(kind, b, c)
-            if kind in (OWN, PREV):
-                w1 = min(w1, k_seq_rows[kind] // W - c * CHUNK)
-                row0 = b * k_seq_rows[kind] + c * CHUNK * W
-                if w1 > w0:
-                    k_view = k_rows[kind][row0 + w0 * W : row0 + w1 * W, :].rearrange(
-                        "(wh a u c) d -> u c a wh d", a=P // 2, u=2, c=2
-                    )
-                    for u in range(2):
-                        for c2 in range(2):
-                            nc.sync.dma_start(out=dst[c2:P:2, u, 2 * w0 : 2 * w1, :], in_=k_view[u, c2])
-                return
-            row0 = b * N + c * CHUNK * W
             if kind == QUERY:
+                row0 = b * N + c * CHUNK * W
                 nc.sync.dma_start(
                     out=dst[:, w0 * QT : w1 * QT, :],
                     in_=q_rows[row0 + w0 * W : row0 + w1 * W, :].rearrange("(a r) d -> r a d", r=P),
                 )
-            else:
+                return
+            w1 = min(w1, seq_rows[kind] // W - c * CHUNK)
+            row0 = b * seq_rows[kind] + c * CHUNK * W
+            if w1 > w0:
                 nc.sync.dma_start(
                     out=dst[:, w0:w1, :, :],
-                    in_=v_rows[row0 + w0 * W : row0 + w1 * W, :].rearrange("(w p j) d -> p w j d", p=P, j=4),
+                    in_=key_rows[kind][row0 + w0 * W : row0 + w1 * W, :].rearrange("(w p j) d -> p w j d", p=P, j=4),
                 )
 
         def load_chunk(c):
             if c >= CHUNKS:
                 return
-            for b in range(B):
-                load(OWN, b, c, 0, CHUNK)
-                load(QUERY, b, c, 0, CHUNK)
-            for kind in ("v", PREV):
+            w0 = 1 if c == 0 else 0
+            for w in range(w0):
                 for b in range(B):
-                    load(kind, b, c, 0, CHUNK)
+                    load(OWN, b, c, w, w + 1)
+                    load(QUERY, b, c, w, w + 1)
+            for b in range(B):
+                load("v", b, c, 0, CHUNK)
+            for b in range(B):
+                load(OWN, b, c, w0, CHUNK)
+                load(QUERY, b, c, w0, CHUNK)
+                load(PREV, b, c, 0, CHUNK)
 
         turned = {}
         live = {}
@@ -200,7 +195,7 @@ def tile_localattention_pa_t_kernel(tc, q_rot, k_own, k_prev, v, out):
                 if kind == QUERY:
                     rows = raw[:, (w % CHUNK) * QT + j, :]
                 else:
-                    rows = raw[:, j // 2, 2 * (w % CHUNK) + j % 2, :]
+                    rows = raw[:, w % CHUNK, j, :]
                 nc.tensor.transpose(t_ps[:, j * P : (j + 1) * P], rows, ident_bf[:])
             live[("t_ps", kind, b, t)] = t_ps
 
@@ -237,27 +232,27 @@ def tile_localattention_pa_t_kernel(tc, q_rot, k_own, k_prev, v, out):
 
         def move_v(b, t):
             for i in range(3):
-                c0, c1 = OWN_COLUMNS[(b, i)]
+                p0, p1 = OWN_PARTITIONS[(b, i)]
                 nc.sync.dma_start(
-                    out=v_part[c0 // 2 : c1 // 2, part_index(b, i, t), :],
-                    in_=v_full[0 : (c1 - c0) // 2, full_index(b, t), :],
+                    out=v_part[p0:p1, part_index(b, i, t), :],
+                    in_=v_full[0 : p1 - p0, full_index(b, t), :],
                 )
 
         def scores(slot):
             kind, t, unit, tiles = slots[slot]
-            s_ps = bank_tile([P, 2, HALF], F32, exp_round[slot] + 0.4)
+            s_ps = bank_tile([P, 4, P], F32, exp_round[slot] + 0.4)
             for b, i in tiles:
-                c0, c1 = (0, HALF) if kind == PREV else OWN_COLUMNS[(b, i)]
+                p0, p1 = (0, P) if kind == PREV else OWN_PARTITIONS[(b, i)]
                 nc.tensor.matmul(
-                    s_ps[:, :, c0:c1],
+                    s_ps[:, :, p0:p1],
                     lhsT=turned[(QUERY, b, t)][:, i * P : (i + 1) * P],
-                    rhs=turned[(kind, b, t)][:].rearrange("d (u c) -> d u c", u=2)[:, :, 0 : c1 - c0],
+                    rhs=turned[(kind, b, t)][:].rearrange("d (j p) -> d j p", j=4)[:, :, 0 : p1 - p0],
                     start=True,
                     stop=(kind == PREV),
                 )
                 if kind == OWN:
                     nc.tensor.matmul(
-                        s_ps[:, :, c1 - DIAG : c1],
+                        s_ps[:, :, p1 - DIAG : p1],
                         lhsT=ident_bf[:],
                         rhs=mask_bf[:],
                         start=False,
@@ -268,24 +263,24 @@ def tile_localattention_pa_t_kernel(tc, q_rot, k_own, k_prev, v, out):
         def row_max(slot):
             kind, t, unit, tiles = slots[slot]
             maxima = small.tile([P, 2], F32, name="own_max" if kind == OWN else "prev_max")
-            columns = [(0, HALF) if kind == PREV else OWN_COLUMNS[tile] for tile in tiles]
+            parts = [(0, P) if kind == PREV else OWN_PARTITIONS[tile] for tile in tiles]
             s_ps = live[("s_ps", slot)]
             for n in range(len(tiles)):
                 live[("max", kind, t, tiles[n])] = maxima[:, n : n + 1]
-            if len(tiles) == 2 and columns[0][1] == HALF // 2:
+            if len(tiles) == 2 and parts[0][1] == P // 2:
                 nc.vector.tensor_reduce(
                     out=maxima[:],
-                    in_=s_ps[:].rearrange("q u (n c) -> q n u c", n=2),
+                    in_=s_ps[:].rearrange("q j (n p) -> q n j p", n=2),
                     axis=AXIS.XY,
                     op=ALU.max,
                     negate=True,
                 )
                 return
             for n in range(len(tiles)):
-                c0, c1 = columns[n]
+                p0, p1 = parts[n]
                 nc.vector.tensor_reduce(
                     out=maxima[:, n : n + 1],
-                    in_=s_ps[:, :, c0:c1],
+                    in_=s_ps[:, :, p0:p1],
                     axis=AXIS.XY,
                     op=ALU.max,
                     negate=True,
@@ -322,15 +317,15 @@ def tile_localattention_pa_t_kernel(tc, q_rot, k_own, k_prev, v, out):
             half = (k - 1) % 2
             pair = (k - 1) // 2
             if half == 0:
-                live[("e", pair)] = work.tile([P, 2, 2, HALF], BF16, align_bytes=64, name="e")
+                live[("e", pair)] = work.tile([P, 2, 2, P, 2], BF16, align_bytes=64, name="e")
             for b, i in tiles:
                 group, place = group_of[(b, i)]
                 if ("rowsum", t, group) not in live:
                     live[("rowsum", t, group)] = small.tile([P, QT, 2], F32, name="rowsum")
-                c0, c1 = (0, HALF) if kind == PREV else OWN_COLUMNS[(b, i)]
+                p0, p1 = (0, P) if kind == PREV else OWN_PARTITIONS[(b, i)]
                 nc.scalar.activation(
-                    out=live[("e", pair)][:, half, :, c0:c1],
-                    in_=live[("s_ps", slot)][:, :, c0:c1],
+                    out=live[("e", pair)][:, half, :, p0:p1, :],
+                    in_=live[("s_ps", slot)][:, :, p0:p1].rearrange("q (u c) p -> q u p c", c=2),
                     func=ACT.Exp,
                     bias=live[("negmax", t, b, i)],
                     scale=1.0,
@@ -338,7 +333,7 @@ def tile_localattention_pa_t_kernel(tc, q_rot, k_own, k_prev, v, out):
                 )
 
         def transpose_e(pair):
-            e_words = live[("e", pair)][:].rearrange("q h u c -> q (h u c)").bitcast(F32)
+            e_words = live[("e", pair)][:].rearrange("q h u p c -> q (h u p c)").bitcast(F32)
             eT_ps = bank_tile([P, 2, 2, P], F32, 2 * pair + 2 + REGROUP_LAG + 0.9)
             for h in range(2):
                 for u in range(2):
@@ -463,10 +458,9 @@ def tile_localattention_pa_t_kernel(tc, q_rot, k_own, k_prev, v, out):
                 for kind, engine in ((OWN, "vector"), (QUERY, "scalar")):
                     prepare_transposes(kind, b, 0, -SCORES_AHEAD)
                     prepare_copy(kind, b, 0, engine)
-                if b == 0:
-                    scores(0)
-                    row_max(0)
-                    negate_max(0)
+            scores(0)
+            row_max(0)
+            negate_max(0)
             for b in range(B):
                 for quarter in range(4):
                     interleave_v(b, 0, quarter)

@@ -40,9 +40,10 @@ OWN_PARTITIONS = {
 }
 GROUPS = ((0, 1), (2, 3, 4))
 BANKS = 8
+VECTOR_PAIRS = 3
 FIRST_WAIT = 1
 SCORES_AHEAD, MAX_AHEAD = 2, 2
-TRANSPOSE_LAG, REGROUP_LAG, QUANTISE_LAG, MULTIPLY_LAG, DIVIDE_LAG = 2, 2, 5, 6, 8
+TRANSPOSE_LAG, REGROUP_LAG, QUANTISE_LAG, MULTIPLY_LAG, DIVIDE_LAG = 2, 2, 5, 5, 9
 PIECES = (
     (OWN, 0, "scalar"),
     (QUERY, 0, "scalar"),
@@ -341,12 +342,14 @@ def tile_localattention_pa_t_kernel(tc, q_rot, k_own, k_prev, v, out):
                     nc.tensor.transpose(eT_ps[:, h, u, :], e_words[:, word0 : word0 + P], ident_f32[:])
             live[("eT_ps", pair)] = eT_ps
 
-        def regroup_e(pair):
+        def regroup_e(pair, engine):
             grouped = work.tile([P, 2 * P * 4], BF16, align_bytes=64, name="grouped")
-            nc.scalar.copy(
-                out=grouped[:].bitcast(F32).rearrange("p (h q u) -> p h q u", h=2, u=2),
-                in_=live[("eT_ps", pair)][:].rearrange("p h u q -> p h q u"),
-            )
+            words = grouped[:].bitcast(F32).rearrange("p (h q u) -> p h q u", h=2, u=2)
+            turned_e = live[("eT_ps", pair)][:].rearrange("p h u q -> p h q u")
+            if engine == "scalar":
+                nc.scalar.copy(out=words, in_=turned_e)
+            else:
+                nc.vector.tensor_copy(out=words, in_=turned_e)
             live[("grouped", pair)] = grouped
 
         def quantise_e(pair):
@@ -422,15 +425,19 @@ def tile_localattention_pa_t_kernel(tc, q_rot, k_own, k_prev, v, out):
         for pair in range(rounds // 2):
             last = 2 * pair + 2
             at("transpose_e", last + TRANSPOSE_LAG, (pair,))
-            at("regroup_e", last + REGROUP_LAG, (pair,))
-            at("quantise_e", last + QUANTISE_LAG, (pair,))
+            if pair < rounds // 2 - VECTOR_PAIRS:
+                at("regroup_e", last + REGROUP_LAG, (pair, "scalar"))
+                at("quantise_e", last + QUANTISE_LAG, (pair,))
+            else:
+                at("regroup_e", last + REGROUP_LAG, (pair, "vector"))
+                at("quantise_e", last + REGROUP_LAG, (pair,))
         for t in range(NW):
             for group in range(len(GROUPS)):
                 unit = GROUPS[group][-1]
                 own = first_slot[t] + sum(1 + (len(UNITS[n]) if t > 0 else 0) for n in range(unit))
                 pair = (exp_round[own] - 1) // 2 + (FIRST_WAIT if t == 0 else 0)
                 for n in range(len(GROUPS[group])):
-                    at("multiply_v", 2 * pair + 2 + MULTIPLY_LAG + n, (t, GROUPS[group][n]))
+                    at("multiply_v", 2 * pair + 2 + MULTIPLY_LAG + 2 * n, (t, GROUPS[group][n]))
                 at("sum_rows", 2 * pair + 4, (t, group))
                 at("invert_sums", 2 * pair + 1 + DIVIDE_LAG, (t, group))
                 at("divide", 2 * pair + 2 + DIVIDE_LAG, (t, group))
@@ -473,6 +480,9 @@ def tile_localattention_pa_t_kernel(tc, q_rot, k_own, k_prev, v, out):
                     multiply_v(*args)
                 for args in plan.get(("transpose_e", k), []):
                     transpose_e(*args)
+                for args in plan.get(("regroup_e", k), []):
+                    if args[1] == "vector":
+                        regroup_e(*args)
                 for args in plan.get(("quantise_e", k), []):
                     quantise_e(*args)
                 if 0 < k + MAX_AHEAD < rounds:
@@ -501,7 +511,8 @@ def tile_localattention_pa_t_kernel(tc, q_rot, k_own, k_prev, v, out):
                     if args[3] == "scalar":
                         prepare_copy(*args)
                 for args in plan.get(("regroup_e", k), []):
-                    regroup_e(*args)
+                    if args[1] == "scalar":
+                        regroup_e(*args)
                 for args in plan.get(("move_v", k), []):
                     move_v(*args)
                 for args in plan.get(("load_chunk", k), []):

@@ -41,7 +41,7 @@ OWN_PARTITIONS = {
 GROUPS = ((0, 1), (2, 3, 4))
 BANKS = 8
 VECTOR_PAIRS = 3
-FIRST_WAIT = 1
+FIRST_WAIT = 2
 SCORES_AHEAD, MAX_AHEAD = 2, 2
 TRANSPOSE_LAG, REGROUP_LAG, QUANTISE_LAG, MULTIPLY_LAG, DIVIDE_LAG = 2, 2, 5, 5, 9
 PIECES = (
@@ -100,36 +100,31 @@ def tile_localattention_pa_t_kernel(tc, q_rot, k_own, k_prev, v, out):
 
 
         ident_bf = const.tile([P, P], BF16)
-        make_identity(nc, ident_bf[:])
-
-        mask_f32 = const.tile([P, P], F32)
-        nc.vector.memset(mask_f32[:], 0.0)
-        nc.gpsimd.affine_select(
-            out=mask_f32[:],
-            in_=mask_f32[:],
-            compare_op=ALU.is_ge,
-            fill=NEG,
-            base=0,
-            pattern=[[-1, P]],
-            channel_multiplier=1,
-        )
-        mask_bf = const.tile([P, 4, DIAG], BF16)
-        nc.vector.tensor_copy(
-            out=mask_bf[:],
-            in_=mask_f32[:].rearrange("r (p j) -> r j p", j=4),
-        )
         ident_f32 = const.tile([P, P], F32)
-        make_identity(nc, ident_f32[:])
-
-        warm = const.tile([P, 1], F32)
-        nc.vector.memset(warm[:], 0.0)
-        warm_out = const.tile([P, 1], F32)
-        nc.scalar.activation(out=warm_out[:], in_=warm[:], func=ACT.Exp)
-
+        mask_f32 = const.tile([P, P], F32)
+        mask_bf = const.tile([P, 4, DIAG], BF16)
         v_full = const.tile([P, B * NW, V_WORDS], I32, align_bytes=64)
-        nc.gpsimd.memset(v_full[:, :, D:], 0)
         v_part = const.tile([P, PART_SLOTS * B * 3, V_WORDS], I32, align_bytes=64)
-        nc.vector.memset(v_part[:], 0)
+        warm = const.tile([P, 1], F32)
+        warm_out = const.tile([P, 1], F32)
+
+        def constants():
+            nc.vector.memset(warm[:], 0.0)
+            nc.vector.memset(mask_f32[:], 0.0)
+            nc.vector.memset(v_part[:], 0)
+            nc.scalar.activation(out=warm_out[:], in_=warm[:], func=ACT.Exp)
+            make_identity(nc, ident_bf[:])
+            nc.gpsimd.affine_select(
+                out=mask_f32[:],
+                in_=mask_f32[:],
+                compare_op=ALU.is_ge,
+                fill=NEG,
+                base=0,
+                pattern=[[-1, P]],
+                channel_multiplier=1,
+            )
+            nc.gpsimd.memset(v_full[:, :, D:], 0)
+            nc.vector.tensor_copy(out=mask_bf[:], in_=mask_f32[:].rearrange("r (p j) -> r j p", j=4))
 
         def full_index(b, t):
             return b * NW + t
@@ -461,6 +456,7 @@ def tile_localattention_pa_t_kernel(tc, q_rot, k_own, k_prev, v, out):
             load_chunk(c)
 
         with tc.manual_schedule():
+            constants()
             for b in range(B):
                 for kind, engine in ((OWN, "vector"), (QUERY, "scalar")):
                     prepare_transposes(kind, b, 0, -SCORES_AHEAD)
@@ -471,15 +467,17 @@ def tile_localattention_pa_t_kernel(tc, q_rot, k_own, k_prev, v, out):
             for b in range(B):
                 for quarter in range(4):
                     interleave_v(b, 0, quarter)
+                if b == 0:
+                    make_identity(nc, ident_f32[:])
             for k in range(-SCORES_AHEAD, rounds + 16):
                 if 0 < k + SCORES_AHEAD < rounds:
                     scores(k + SCORES_AHEAD)
-                for args in plan.get(("prepare", k), []):
-                    prepare_transposes(args[0], args[1], args[2], k)
                 for args in plan.get(("multiply_v", k), []):
                     multiply_v(*args)
                 for args in plan.get(("transpose_e", k), []):
                     transpose_e(*args)
+                for args in plan.get(("prepare", k), []):
+                    prepare_transposes(args[0], args[1], args[2], k)
                 for args in plan.get(("regroup_e", k), []):
                     if args[1] == "vector":
                         regroup_e(*args)
@@ -507,12 +505,12 @@ def tile_localattention_pa_t_kernel(tc, q_rot, k_own, k_prev, v, out):
                     interleave_v(*args)
                 if k in exp_item:
                     exponentials(k)
-                for args in plan.get(("prepare", k), []):
-                    if args[3] == "scalar":
-                        prepare_copy(*args)
                 for args in plan.get(("regroup_e", k), []):
                     if args[1] == "scalar":
                         regroup_e(*args)
+                for args in plan.get(("prepare", k), []):
+                    if args[3] == "scalar":
+                        prepare_copy(*args)
                 for args in plan.get(("move_v", k), []):
                     move_v(*args)
                 for args in plan.get(("load_chunk", k), []):

@@ -23,7 +23,7 @@ NEG = -1.0e30
 LOWEST = -3.0e38
 CHUNK = 2
 CHUNKS = NW // CHUNK
-LOAD_AHEAD = 2
+LOAD_AHEAD = 3
 V_WORDS = D + D // 4
 PART_SLOTS = 3
 
@@ -41,7 +41,7 @@ OWN_PARTITIONS = {
 GROUPS = ((0, 1), (2, 3, 4))
 BANKS = 8
 VECTOR_PAIRS = 3
-FIRST_WAIT = 2
+FIRST_WAIT = 1
 SCORES_AHEAD, MAX_AHEAD = 2, 2
 TRANSPOSE_LAG, REGROUP_LAG, QUANTISE_LAG, MULTIPLY_LAG, DIVIDE_LAG = 2, 2, 5, 5, 9
 PIECES = (
@@ -165,20 +165,17 @@ def tile_localattention_pa_t_kernel(tc, q_rot, k_own, k_prev, v, out):
                     in_=key_rows[kind][row0 + w0 * W : row0 + w1 * W, :].rearrange("(w p j) d -> p w j d", p=P, j=4),
                 )
 
-        def load_chunk(c):
-            if c >= CHUNKS:
+        def load_pair(t):
+            if t >= NW:
                 return
-            w0 = 1 if c == 0 else 0
-            for w in range(w0):
-                for b in range(B):
-                    load(OWN, b, c, w, w + 1)
-                    load(QUERY, b, c, w, w + 1)
+            c, w = divmod(t, CHUNK)
             for b in range(B):
-                load("v", b, c, 0, CHUNK)
+                load(OWN, b, c, w, w + 1)
+                load(QUERY, b, c, w, w + 1)
+                if t > 0:
+                    load(PREV, b, (t - 1) // CHUNK, (t - 1) % CHUNK, (t - 1) % CHUNK + 1)
             for b in range(B):
-                load(OWN, b, c, w0, CHUNK)
-                load(QUERY, b, c, w0, CHUNK)
-                load(PREV, b, c, 0, CHUNK)
+                load("v", b, c, w, w + 1)
 
         turned = {}
         live = {}
@@ -448,12 +445,11 @@ def tile_localattention_pa_t_kernel(tc, q_rot, k_own, k_prev, v, out):
                     at("interleave_v", k, (b, t, quarter))
                 at("quantise_v", k + 1, (b, t))
                 at("move_v", k + 1, (b, t))
-            if t % CHUNK == 0:
-                at("load_chunk", k0, (t // CHUNK + LOAD_AHEAD,))
-        at("load_chunk", 6, (LOAD_AHEAD,))
+            at("load_pair", k0, (t + LOAD_AHEAD,))
+        at("load_pair", 2, (LOAD_AHEAD,))
 
-        for c in range(LOAD_AHEAD):
-            load_chunk(c)
+        for t in range(LOAD_AHEAD):
+            load_pair(t)
 
         with tc.manual_schedule():
             constants()
@@ -513,5 +509,5 @@ def tile_localattention_pa_t_kernel(tc, q_rot, k_own, k_prev, v, out):
                         prepare_copy(*args)
                 for args in plan.get(("move_v", k), []):
                     move_v(*args)
-                for args in plan.get(("load_chunk", k), []):
-                    load_chunk(*args)
+                for args in plan.get(("load_pair", k), []):
+                    load_pair(*args)

@@ -102,7 +102,7 @@ def tile_localattention_pa_t_kernel(tc, q_rot, k_own, k_prev, v, out):
         ident_bf = const.tile([P, P], BF16)
         ident_f32 = const.tile([P, P], F32)
         mask_f32 = const.tile([P, P], F32)
-        mask_bf = const.tile([P, 4, DIAG], BF16)
+        mask_bf = const.tile([P, 4, 2, DIAG], BF16)
         v_full = const.tile([P, B * NW, V_WORDS], I32, align_bytes=64)
         v_part = const.tile([P, PART_SLOTS * B * 3, V_WORDS], I32, align_bytes=64)
         warm = const.tile([P, 1], F32)
@@ -124,7 +124,8 @@ def tile_localattention_pa_t_kernel(tc, q_rot, k_own, k_prev, v, out):
                 channel_multiplier=1,
             )
             nc.gpsimd.memset(v_full[:, :, D:], 0)
-            nc.vector.tensor_copy(out=mask_bf[:], in_=mask_f32[:].rearrange("r (p j) -> r j p", j=4))
+            for n in range(2):
+                nc.vector.tensor_copy(out=mask_bf[:, :, n, :], in_=mask_f32[:].rearrange("r (p j) -> r j p", j=4))
 
         def full_index(b, t):
             return b * NW + t
@@ -234,23 +235,30 @@ def tile_localattention_pa_t_kernel(tc, q_rot, k_own, k_prev, v, out):
         def scores(slot):
             kind, t, unit, tiles = slots[slot]
             s_ps = bank_tile([P, 4, P], F32, exp_round[slot] + 0.4)
-            for b, i in tiles:
+            for n in range(len(tiles)):
+                b, i = tiles[n]
                 p0, p1 = (0, P) if kind == PREV else OWN_PARTITIONS[(b, i)]
                 nc.tensor.matmul(
                     s_ps[:, :, p0:p1],
                     lhsT=turned[(QUERY, b, t)][:, i * P : (i + 1) * P],
                     rhs=turned[(kind, b, t)][:].rearrange("d (j p) -> d j p", j=4)[:, :, 0 : p1 - p0],
-                    start=True,
+                    start=(n == 0),
                     stop=(kind == PREV),
                 )
-                if kind == OWN:
-                    nc.tensor.matmul(
-                        s_ps[:, :, p1 - DIAG : p1],
-                        lhsT=ident_bf[:],
-                        rhs=mask_bf[:],
-                        start=False,
-                        stop=True,
-                    )
+            if kind == OWN:
+                if len(tiles) == 1:
+                    blocks = s_ps[:, :, P - DIAG :]
+                elif OWN_PARTITIONS[tiles[0]][0] == 0:
+                    blocks = s_ps[:].rearrange("q j (n p) -> q j n p", n=2)[:, :, :, P // 2 - DIAG :]
+                else:
+                    blocks = s_ps[:, :, P - 2 * DIAG :].rearrange("q j (n p) -> q j n p", n=2)
+                nc.tensor.matmul(
+                    blocks,
+                    lhsT=ident_bf[:],
+                    rhs=mask_bf[:, :, 0, :] if len(tiles) == 1 else mask_bf[:],
+                    start=False,
+                    stop=True,
+                )
             live[("s_ps", slot)] = s_ps
 
         def row_max(slot):

from contextlib import ExitStack

import concourse.mybir as mybir
from concourse.masks import make_identity

BF16 = mybir.dt.bfloat16
F32 = mybir.dt.float32
I32 = mybir.dt.int32
U32 = mybir.dt.uint32
U8 = mybir.dt.uint8
FP8X4 = mybir.dt.float8_e4m3fn_x4
ALU = mybir.AluOpType
ACT = mybir.ActivationFunctionType
AXIS = mybir.AxisListType

B, N, W, D = 2, 8192, 512, 128
P = 128
NW = N // W
QT = W // P
DIAG = P // 4
PREV, OWN, QUERY = 0, 1, 2
NEG = -1.0e30
LOWEST = -3.0e38
CHUNK = 2
CHUNKS = NW // CHUNK
LOAD_AHEAD = 3
V_WORDS = D + D // 4
PART_SLOTS = 3

UNITS = (((0, 0), (0, 2)), ((1, 0), (1, 2)), ((0, 1), (1, 1)), ((0, 3),), ((1, 3),))
OWN_PARTITIONS = {
    (0, 2): (0, 96),
    (1, 2): (0, 96),
    (0, 0): (96, 128),
    (1, 0): (96, 128),
    (0, 1): (0, 64),
    (1, 1): (64, 128),
    (0, 3): (0, 128),
    (1, 3): (0, 128),
}
GROUPS = ((0, 1), (2, 3, 4))
BANKS = 8
VECTOR_PAIRS = 3
FIRST_WAIT = 1
SCORES_AHEAD, MAX_AHEAD = 2, 2
TRANSPOSE_LAG, REGROUP_LAG, QUANTISE_LAG, MULTIPLY_LAG, DIVIDE_LAG = 2, 2, 5, 5, 9
PIECES = (
    (OWN, 0, "scalar"),
    (QUERY, 0, "scalar"),
    (PREV, 0, "vector"),
    (OWN, 1, "vector"),
    (QUERY, 1, "scalar"),
    (PREV, 1, "vector"),
)

FLOPS = 2 * 2 * B * (W * W + (NW - 1) * W * 2 * W) * D


def tile_localattention_pa_t_kernel(tc, q_rot, k_own, k_prev, v, out):
    nc = tc.nc
    q_rows = q_rot.flatten_outer_dims()
    key_rows = {
        OWN: k_own.flatten_outer_dims(),
        PREV: k_prev.flatten_outer_dims(),
        "v": v.flatten_outer_dims(),
    }
    seq_rows = {OWN: N, PREV: N - W, "v": N}
    out_rows = out.flatten_outer_dims()

    slots = []
    first_slot = []
    exp_item = {}
    for t in range(NW):
        first_slot.append(len(slots))
        for unit in range(len(UNITS)):
            own_slot = len(slots)
            slots.append((OWN, t, unit, UNITS[unit]))
            if t > 0:
                for tile in UNITS[unit]:
                    exp_item[len(slots)] = len(slots)
                    slots.append((PREV, t, unit, (tile,)))
            exp_item[len(slots)] = own_slot
    first_slot.append(len(slots))
    rounds = len(slots)
    exp_round = {slot: k for k, slot in exp_item.items()}

    with ExitStack() as ctx:
        const = ctx.enter_context(tc.tile_pool(name="const", bufs=1))
        turned_pool = ctx.enter_context(tc.tile_pool(name="turned_pool", bufs=2))
        work = ctx.enter_context(tc.tile_pool(name="work", bufs=4))
        codes_pool = ctx.enter_context(tc.tile_pool(name="codes_pool", bufs=10))
        small = ctx.enter_context(tc.tile_pool(name="small", bufs=14))
        psum = ctx.enter_context(tc.psum_pool(name="psum", bufs=1))
        free_from = [-100.0] * BANKS

        def bank_tile(shape, dtype, last_read):
            bank = free_from.index(min(free_from))
            free_from[bank] = last_read
            return psum.tile(shape, dtype, name="bank_%d" % bank)


        ident_bf = const.tile([P, P], BF16)
        ident_f32 = const.tile([P, P], F32)
        mask_f32 = const.tile([P, P], F32)
        mask_bf = const.tile([P, 4, 2, DIAG], BF16)
        v_full = const.tile([P, B * NW, V_WORDS], I32, align_bytes=64)
        v_part = const.tile([P, PART_SLOTS * B * 3, V_WORDS], I32, align_bytes=64)
        warm = const.tile([P, 1], F32)
        warm_out = const.tile([P, 1], F32)

        def constants():
            nc.vector.memset(warm[:], 0.0)
            nc.vector.memset(mask_f32[:], 0.0)
            nc.vector.memset(v_part[:], 0)
            nc.scalar.activation(out=warm_out[:], in_=warm[:], func=ACT.Exp)
            make_identity(nc, ident_bf[:])
            nc.gpsimd.affine_select(
                out=mask_f32[:],
                in_=mask_f32[:],
                compare_op=ALU.is_ge,
                fill=NEG,
                base=0,
                pattern=[[-1, P]],
                channel_multiplier=1,
            )
            nc.gpsimd.memset(v_full[:, :, D:], 0)
            for n in range(2):
                nc.vector.tensor_copy(out=mask_bf[:, :, n, :], in_=mask_f32[:].rearrange("r (p j) -> r j p", j=4))

        def full_index(b, t):
            return b * NW + t

        def part_index(b, i, t):
            return ((t % PART_SLOTS) * B + b) * 3 + i

        def codes_of(words):
            return words[:, 0:D].bitcast(FP8X4)

        def scales_of(words):
            return words[:, D:].bitcast(U8)

        loaded = {}

        def chunk_tile(kind, b, c):
            if (kind, b, c) not in loaded:
                if kind == QUERY:
                    loaded[(kind, b, c)] = const.tile([P, CHUNK * QT, D], BF16, name="q_raw_%d_%d" % (b, c))
                else:
                    loaded[(kind, b, c)] = const.tile([P, CHUNK, 4, D], BF16, name="rows_%s_%d_%d" % (kind, b, c))
            return loaded[(kind, b, c)]

        def load(kind, b, c, w0, w1):
            dst = chunk_tile(kind, b, c)
            if kind == QUERY:
                row0 = b * N + c * CHUNK * W
                nc.sync.dma_start(
                    out=dst[:, w0 * QT : w1 * QT, :],
                    in_=q_rows[row0 + w0 * W : row0 + w1 * W, :].rearrange("(a r) d -> r a d", r=P),
                )
                return
            w1 = min(w1, seq_rows[kind] // W - c * CHUNK)
            row0 = b * seq_rows[kind] + c * CHUNK * W
            if w1 > w0:
                nc.sync.dma_start(
                    out=dst[:, w0:w1, :, :],
                    in_=key_rows[kind][row0 + w0 * W : row0 + w1 * W, :].rearrange("(w p j) d -> p w j d", p=P, j=4),
                )

        def load_pair(t):
            if t >= NW:
                return
            c, w = divmod(t, CHUNK)
            for b in range(B):
                load(OWN, b, c, w, w + 1)
                load(QUERY, b, c, w, w + 1)
                if t > 0:
                    load(PREV, b, (t - 1) // CHUNK, (t - 1) % CHUNK, (t - 1) % CHUNK + 1)
            for b in range(B):
                load("v", b, c, w, w + 1)

        turned = {}
        live = {}

        def prepare_transposes(kind, b, t, k):
            w = t - 1 if kind == PREV else t
            raw = chunk_tile(kind, b, w // CHUNK)
            t_ps = bank_tile([P, W], BF16, k + 0.5)
            for j in range(QT):
                if kind == QUERY:
                    rows = raw[:, (w % CHUNK) * QT + j, :]
                else:
                    rows = raw[:, w % CHUNK, j, :]
                nc.tensor.transpose(t_ps[:, j * P : (j + 1) * P], rows, ident_bf[:])
            live[("t_ps", kind, b, t)] = t_ps

        def prepare_copy(kind, b, t, engine):
            t_sb = turned_pool.tile([P, W], BF16, name="turned_%d_%d" % (kind, b))
            turned[(kind, b, t)] = t_sb
            t_ps = live[("t_ps", kind, b, t)]
            if engine == "scalar":
                nc.scalar.copy(out=t_sb[:].bitcast(F32), in_=t_ps[:].bitcast(F32))
            else:
                nc.vector.tensor_copy(out=t_sb[:].bitcast(F32), in_=t_ps[:].bitcast(F32))

        def interleave_v(b, t, quarter):
            if quarter == 0:
                live[("v_grouped", b, t)] = work.tile([P, D, 4], BF16, align_bytes=64, name="v_grouped")
            v_raw = chunk_tile("v", b, t // CHUNK)
            features = slice(quarter * (D // 4), (quarter + 1) * (D // 4))
            nc.gpsimd.tensor_scalar(
                out=live[("v_grouped", b, t)][:, features, :],
                in0=v_raw[:, t % CHUNK, :, features].rearrange("p j d -> p d j"),
                scalar1=1.0,
                scalar2=0.0,
                op0=ALU.mult,
                op1=ALU.add,
            )

        def quantise_v(b, t):
            words = v_full[:, full_index(b, t), :]
            nc.vector.quantize_mx(
                out=codes_of(words),
                scales=scales_of(words),
                in_=live[("v_grouped", b, t)][:].rearrange("p d j -> p (d j)"),
            )

        def move_v(b, t):
            for i in range(3):
                p0, p1 = OWN_PARTITIONS[(b, i)]
                nc.sync.dma_start(
                    out=v_part[p0:p1, part_index(b, i, t), :],
                    in_=v_full[0 : p1 - p0, full_index(b, t), :],
                )

        def scores(slot):
            kind, t, unit, tiles = slots[slot]
            s_ps = bank_tile([P, 4, P], F32, exp_round[slot] + 0.4)
            for n in range(len(tiles)):
                b, i = tiles[n]
                p0, p1 = (0, P) if kind == PREV else OWN_PARTITIONS[(b, i)]
                nc.tensor.matmul(
                    s_ps[:, :, p0:p1],
                    lhsT=turned[(QUERY, b, t)][:, i * P : (i + 1) * P],
                    rhs=turned[(kind, b, t)][:].rearrange("d (j p) -> d j p", j=4)[:, :, 0 : p1 - p0],
                    start=(n == 0),
                    stop=(kind == PREV),
                )
            if kind == OWN:
                if len(tiles) == 1:
                    blocks = s_ps[:, :, P - DIAG :]
                elif OWN_PARTITIONS[tiles[0]][0] == 0:
                    blocks = s_ps[:].rearrange("q j (n p) -> q j n p", n=2)[:, :, :, P // 2 - DIAG :]
                else:
                    blocks = s_ps[:, :, P - 2 * DIAG :].rearrange("q j (n p) -> q j n p", n=2)
                nc.tensor.matmul(
                    blocks,
                    lhsT=ident_bf[:],
                    rhs=mask_bf[:, :, 0, :] if len(tiles) == 1 else mask_bf[:],
                    start=False,
                    stop=True,
                )
            live[("s_ps", slot)] = s_ps

        def row_max(slot):
            kind, t, unit, tiles = slots[slot]
            maxima = small.tile([P, 2], F32, name="own_max" if kind == OWN else "prev_max")
            parts = [(0, P) if kind == PREV else OWN_PARTITIONS[tile] for tile in tiles]
            s_ps = live[("s_ps", slot)]
            for n in range(len(tiles)):
                live[("max", kind, t, tiles[n])] = maxima[:, n : n + 1]
            if len(tiles) == 2 and parts[0][1] == P // 2:
                nc.vector.tensor_reduce(
                    out=maxima[:],
                    in_=s_ps[:].rearrange("q j (n p) -> q n j p", n=2),
                    axis=AXIS.XY,
                    op=ALU.max,
                    negate=True,
                )
                return
            for n in range(len(tiles)):
                p0, p1 = parts[n]
                nc.vector.tensor_reduce(
                    out=maxima[:, n : n + 1],
                    in_=s_ps[:, :, p0:p1],
                    axis=AXIS.XY,
                    op=ALU.max,
                    negate=True,
                )

        def negate_max(slot):
            kind, t, unit, tiles = slots[slot]
            for b, i in tiles:
                if t == 0:
                    live[("negmax", t, b, i)] = live[("max", OWN, t, (b, i))]
                elif kind == PREV:
                    negmax = small.tile([P, 1], F32, name="negmax")
                    nc.gpsimd.tensor_scalar(
                        out=negmax[:],
                        in0=live[("max", PREV, t, (b, i))],
                        scalar1=live[("max", OWN, t, (b, i))],
                        scalar2=LOWEST,
                        op0=ALU.min,
                        op1=ALU.max,
                    )
                    live[("negmax", t, b, i)] = negmax[:]

        group_of = {}
        group_tiles = []
        for group in range(len(GROUPS)):
            members = [tile for unit in GROUPS[group] for tile in UNITS[unit]]
            group_tiles.append(members)
            for place in range(len(members)):
                group_of[members[place]] = (group, place)

        def exponentials(k):
            slot = exp_item[k]
            kind, t, unit, tiles = slots[slot]
            half = (k - 1) % 2
            pair = (k - 1) // 2
            if half == 0:
                live[("e", pair)] = work.tile([P, 2, 2, P, 2], BF16, align_bytes=64, name="e")
            for b, i in tiles:
                group, place = group_of[(b, i)]
                if ("rowsum", t, group) not in live:
                    live[("rowsum", t, group)] = small.tile([P, QT, 2], F32, name="rowsum")
                p0, p1 = (0, P) if kind == PREV else OWN_PARTITIONS[(b, i)]
                nc.scalar.activation(
                    out=live[("e", pair)][:, half, :, p0:p1, :],
                    in_=live[("s_ps", slot)][:, :, p0:p1].rearrange("q (u c) p -> q u p c", c=2),
                    func=ACT.Exp,
                    bias=live[("negmax", t, b, i)],
                    scale=1.0,
                    accum_out=live[("rowsum", t, group)][:, place, kind : kind + 1],
                )

        def transpose_e(pair):
            e_words = live[("e", pair)][:].rearrange("q h u p c -> q (h u p c)").bitcast(F32)
            eT_ps = bank_tile([P, 2, 2, P], F32, 2 * pair + 2 + REGROUP_LAG + 0.9)
            for h in range(2):
                for u in range(2):
                    word0 = (2 * h + u) * P
                    nc.tensor.transpose(eT_ps[:, h, u, :], e_words[:, word0 : word0 + P], ident_f32[:])
            live[("eT_ps", pair)] = eT_ps

        def regroup_e(pair, engine):
            grouped = work.tile([P, 2 * P * 4], BF16, align_bytes=64, name="grouped")
            words = grouped[:].bitcast(F32).rearrange("p (h q u) -> p h q u", h=2, u=2)
            turned_e = live[("eT_ps", pair)][:].rearrange("p h u q -> p h q u")
            if engine == "scalar":
                nc.scalar.copy(out=words, in_=turned_e)
            else:
                nc.vector.tensor_copy(out=words, in_=turned_e)
            live[("grouped", pair)] = grouped

        def quantise_e(pair):
            e_codes = codes_pool.tile([P, 2 * P], U32, align_bytes=64, name="e_codes")
            e_scales = codes_pool.tile([P, 2 * P], U8, align_bytes=64, name="e_scales")
            nc.vector.quantize_mx(out=e_codes[:].bitcast(FP8X4), scales=e_scales[:], in_=live[("grouped", pair)][:])
            live[("e_codes", pair)] = e_codes
            live[("e_scales", pair)] = e_scales

        def multiply_v(t, unit):
            for b, i in UNITS[unit]:
                group, place = group_of[(b, i)]
                if place == 0:
                    live[("o_ps", t, group)] = bank_tile([P, QT, D], F32, divide_round[(t, group)] + 0.9)
                passes = []
                own = first_slot[t] + sum(1 + (len(UNITS[n]) if t > 0 else 0) for n in range(unit))
                if t > 0:
                    prev = own + 1 + UNITS[unit].index((b, i))
                    passes.append((exp_round[prev], v_full[:, full_index(b, t - 1), :]))
                own_words = v_full[:, full_index(b, t), :] if i == 3 else v_part[:, part_index(b, i, t), :]
                passes.append((exp_round[own], own_words))
                for n in range(len(passes)):
                    k, words = passes[n]
                    half = (k - 1) % 2
                    pair = (k - 1) // 2
                    nc.tensor.matmul_mx(
                        out=live[("o_ps", t, group)][:, place, :],
                        lhsT=live[("e_codes", pair)][:, half * P : (half + 1) * P].bitcast(FP8X4),
                        lhsT_scale=live[("e_scales", pair)][:, half * P : (half + 1) * P],
                        rhs=codes_of(words),
                        rhs_scale=scales_of(words),
                        start=(n == 0),
                        stop=(n == len(passes) - 1),
                    )

        def sum_rows(t, group):
            rowsum = live[("rowsum", t, group)]
            if t > 0:
                total = small.tile([P, QT], F32, name="total")
                nc.gpsimd.tensor_tensor(out=total[:], in0=rowsum[:, :, PREV], in1=rowsum[:, :, OWN], op=ALU.add)
                live[("total", t, group)] = total[:]
            else:
                live[("total", t, group)] = rowsum[:, :, OWN]

        def invert_sums(t, group):
            recip = small.tile([P, QT], F32, name="recip")
            nc.vector.reciprocal(out=recip[:], in_=live[("total", t, group)])
            live[("recip", t, group)] = recip

        def divide_and_store(t, group):
            o_sb = work.tile([P, QT, D], F32, name="o_sb")
            nc.vector.tensor_tensor(
                out=o_sb[:],
                in0=live[("o_ps", t, group)][:],
                in1=live[("recip", t, group)][:].unsqueeze(2).to_broadcast([P, QT, D]),
                op=ALU.mult,
            )
            for b in range(B):
                places = [place for place in range(QT) if group_tiles[group][place][0] == b]
                i = group_tiles[group][places[0]][1]
                row0 = b * N + t * W
                nc.sync.dma_start(
                    out=out_rows[row0 : row0 + W, :].rearrange("(a r) d -> r a d", r=P)[:, i::2, :],
                    in_=o_sb[:, places[0] : places[1] + 1 : places[1] - places[0], :],
                )

        divide_round = {}
        plan = {}

        def at(stage, k, args):
            plan.setdefault((stage, k), []).append(args)

        for pair in range(rounds // 2):
            last = 2 * pair + 2
            at("transpose_e", last + TRANSPOSE_LAG, (pair,))
            if pair < rounds // 2 - VECTOR_PAIRS:
                at("regroup_e", last + REGROUP_LAG, (pair, "scalar"))
                at("quantise_e", last + QUANTISE_LAG, (pair,))
            else:
                at("regroup_e", last + REGROUP_LAG, (pair, "vector"))
                at("quantise_e", last + REGROUP_LAG, (pair,))
        for t in range(NW):
            for group in range(len(GROUPS)):
                unit = GROUPS[group][-1]
                own = first_slot[t] + sum(1 + (len(UNITS[n]) if t > 0 else 0) for n in range(unit))
                pair = (exp_round[own] - 1) // 2 + (FIRST_WAIT if t == 0 else 0)
                for n in range(len(GROUPS[group])):
                    at("multiply_v", 2 * pair + 2 + MULTIPLY_LAG + 2 * n, (t, GROUPS[group][n]))
                at("sum_rows", 2 * pair + 4, (t, group))
                at("invert_sums", 2 * pair + 1 + DIVIDE_LAG, (t, group))
                at("divide", 2 * pair + 2 + DIVIDE_LAG, (t, group))
                divide_round[(t, group)] = 2 * pair + 2 + DIVIDE_LAG
        for t in range(1, NW):
            k0, k1 = first_slot[t - 1], first_slot[t]
            for n in range(len(PIECES)):
                kind, b, engine = PIECES[n]
                at("prepare", k0 + n * (k1 - k0) // len(PIECES), (kind, b, t, engine))
            for b in range(B):
                for quarter in range(4):
                    k = k0 + (4 * b + quarter) * (k1 - k0) // 8
                    at("interleave_v", k, (b, t, quarter))
                at("quantise_v", k + 1, (b, t))
                at("move_v", k + 1, (b, t))
            at("load_pair", k0, (t + LOAD_AHEAD,))
        at("load_pair", 2, (LOAD_AHEAD,))

        for t in range(LOAD_AHEAD):
            load_pair(t)

        with tc.manual_schedule():
            constants()
            for b in range(B):
                for kind, engine in ((OWN, "vector"), (QUERY, "scalar")):
                    prepare_transposes(kind, b, 0, -SCORES_AHEAD)
                    prepare_copy(kind, b, 0, engine)
            scores(0)
            row_max(0)
            negate_max(0)
            for b in range(B):
                for quarter in range(4):
                    interleave_v(b, 0, quarter)
                if b == 0:
                    make_identity(nc, ident_f32[:])
            for k in range(-SCORES_AHEAD, rounds + 16):
                if 0 < k + SCORES_AHEAD < rounds:
                    scores(k + SCORES_AHEAD)
                for args in plan.get(("multiply_v", k), []):
                    multiply_v(*args)
                for args in plan.get(("transpose_e", k), []):
                    transpose_e(*args)
                for args in plan.get(("prepare", k), []):
                    prepare_transposes(args[0], args[1], args[2], k)
                for args in plan.get(("regroup_e", k), []):
                    if args[1] == "vector":
                        regroup_e(*args)
                for args in plan.get(("quantise_e", k), []):
                    quantise_e(*args)
                if 0 < k + MAX_AHEAD < rounds:
                    row_max(k + MAX_AHEAD)
                for args in plan.get(("prepare", k), []):
                    if args[3] == "vector":
                        prepare_copy(*args)
                for args in plan.get(("quantise_v", k), []):
                    quantise_v(*args)
                if k in (0, 1):
                    quantise_v(k, 0)
                    move_v(k, 0)
                for args in plan.get(("invert_sums", k), []):
                    invert_sums(*args)
                for args in plan.get(("divide", k), []):
                    divide_and_store(*args)
                if 0 < k + MAX_AHEAD < rounds:
                    negate_max(k + MAX_AHEAD)
                for args in plan.get(("sum_rows", k), []):
                    sum_rows(*args)
                for args in plan.get(("interleave_v", k), []):
                    interleave_v(*args)
                if k in exp_item:
                    exponentials(k)
                for args in plan.get(("regroup_e", k), []):
                    if args[1] == "scalar":
                        regroup_e(*args)
                for args in plan.get(("prepare", k), []):
                    if args[3] == "scalar":
                        prepare_copy(*args)
                for args in plan.get(("move_v", k), []):
                    move_v(*args)
                for args in plan.get(("load_pair", k), []):
                    load_pair(*args)
